import numpy as np
import ml_dtypes


BF16 = ml_dtypes.bfloat16


def bf(x):
    return np.asarray(x, np.float32).astype(BF16)


def f64(x):
    return np.asarray(x).astype(np.float64)


E2M1 = np.array([0.0, 0.5, 1.0, 1.5, 2.0, 3.0, 4.0, 6.0, -0.0, -0.5, -1.0, -1.5, -2.0, -3.0, -4.0, -6.0])


def pack_weight(w, fmt):
    k, n = w.shape
    w = f64(bf(w)).reshape(k // 32, 32, n)
    amax = np.abs(w).max(1)
    if fmt == "e4m3":
        byte = np.frexp(amax)[1] - 1 + 127 - 7
    else:
        mant, ex = np.frexp(amax / 6.0)
        byte = np.where(mant > 0.5, ex, ex - 1) + 127
    byte = np.clip(np.where(amax > 0, byte, 1), 1, 254)
    scaled = (w * np.exp2(127.0 - byte)[:, None, :]).reshape(k, n).astype(np.float32)
    by_word = np.ascontiguousarray(scaled.reshape(k // 512, 128, 4, n).transpose(0, 1, 3, 2))
    if fmt == "e4m3":
        words = by_word.astype(ml_dtypes.float8_e4m3fn).view(np.uint8)
    else:
        c = by_word.astype(ml_dtypes.float4_e2m1fn).view(np.uint8) & 0xF
        words = c[..., 0::2] | (c[..., 1::2] << 4)
    return np.ascontiguousarray(words), np.ascontiguousarray(byte.astype(np.uint8).reshape(k // 512, 16, n))


def unpack_weight(words, scales, fmt):
    g, p, n, _ = words.shape
    if fmt == "e4m3":
        vals = np.ascontiguousarray(words).view(ml_dtypes.float8_e4m3fn).astype(np.float64)
    else:
        nib = np.empty((g, p, n, 4), np.uint8)
        nib[..., 0::2] = words & 0xF
        nib[..., 1::2] = words >> 4
        vals = E2M1[nib]
    vals = vals * np.repeat(np.exp2(scales.astype(np.float64) - 127.0), 8, axis=1)[..., None]
    return vals.transpose(0, 1, 3, 2).reshape(g * 512, n)

def pack4(w):
    words, scales = pack_weight(w, "e2m1")
    return words.reshape(words.shape[0], 128, -1), scales


def unpack4(words, scales):
    return unpack_weight(words.reshape(words.shape[0], 128, -1, 2), scales, "e2m1")


def kspread(k):
    return np.exp2(np.repeat(np.random.randint(-6, 7, k // 32), 32).astype(np.float64))


B, T, C, H, D, R = 1, 1024, 1024, 16, 128, 512
EPS = 1e-6
THETA = 10000.0


def rmsnorm(v, w):
    var = np.mean(v * v, axis=-1, keepdims=True)
    return v * (1.0 / np.sqrt(var + EPS)) * w


def rope(v, cos, sin):
    re, im = v[..., 0::2], v[..., 1::2]
    c, s = cos[None, :, None, :], sin[None, :, None, :]
    return np.stack([re * c - im * s, re * s + im * c], axis=-1).reshape(v.shape)


def setup_inputs():
    s = kspread(C)
    ang = np.outer(np.arange(T), 1.0 / THETA ** (np.arange(0, D, 2) / D))
    x = np.random.standard_normal((B, T, C)) * s
    x_words, x_scales = pack4(np.ascontiguousarray(x.reshape(B * T, C).T))
    wq = np.random.standard_normal((H * D, C)) / np.sqrt(C) / s[None, :]
    wq_words, wq_scales = pack4(np.ascontiguousarray(wq.T))
    q_norm_w = bf(1.0 + 0.1 * np.random.standard_normal(D))
    return {"x_words": x_words, "x_scales": x_scales,
            "wq_words": wq_words, "wq_scales": wq_scales,
            "q_norm_w": q_norm_w,
            "freqs_cos": bf(np.cos(ang)), "freqs_sin": bf(np.sin(ang))}


def reference(x_words, x_scales, wq_words, wq_scales, q_norm_w, freqs_cos, freqs_sin):
    xq = (unpack4(x_words, x_scales).T.reshape(B, T, C) @ unpack4(wq_words, wq_scales)).reshape(B, T, H, D)
    return rope(rmsnorm(xq, f64(q_norm_w)), f64(freqs_cos), f64(freqs_sin))

@@ -1,0 +1,209 @@
+from contextlib import ExitStack
+import math
+
+import concourse.mybir as mybir
+
+T, C, H, D = 1024, 1024, 16, 128
+N = H * D
+EPS = 1e-6
+FLOPS = 2 * T * C * N
+
+F32 = mybir.dt.float32
+BF16 = mybir.dt.bfloat16
+U8 = mybir.dt.uint8
+I32 = mybir.dt.int32
+FP4 = mybir.dt.float4_e2m1fn_x4
+AF = mybir.ActivationFunctionType
+ALU = mybir.AluOpType
+
+P = 128
+G = C // 512
+NT = T // P
+NB = 512
+NBK = N // NB
+HB = NB // D
+J = D // 2
+
+Q_BANKS = ()
+
+
+def tile_mla_pb_kernel(tc, x_words, x_scales, wq_words, wq_scales, q_norm_w, freqs_cos, freqs_sin, out):
+    nc = tc.nc
+    out2 = out.rearrange("b t h d -> (b t) (h d)")
+
+    with ExitStack() as ctx:
+        const = ctx.enter_context(tc.tile_pool(name="const", bufs=1))
+        work = ctx.enter_context(tc.tile_pool(name="work", bufs=4))
+        stat = ctx.enter_context(tc.tile_pool(name="stat", bufs=3))
+        psum = ctx.enter_context(tc.psum_pool(name="psum", bufs=8))
+        ctx.enter_context(tc.manual_schedule())
+
+        xc = const.tile([P, G, 2 * T], U8, name="xc", align_bytes=64)
+        xs = const.tile([P, G, T], U8, name="xs", align_bytes=64)
+        ws = const.tile([P, G, N], U8, name="ws", align_bytes=64)
+        wc = []
+        for n in range(NBK):
+            wc_n = const.tile([P, G, 2 * NB], U8, name="wc%d" % n, align_bytes=64)
+            wc.append(wc_n)
+        cos_sb = const.tile([P, NT, J], BF16, name="cos_sb")
+        sin_sb = const.tile([P, NT, J], BF16, name="sin_sb")
+        wrow = const.tile([P, 2 * D], BF16, name="wrow")
+        ones = const.tile([P, P], BF16, name="ones")
+        eps_t = const.tile([P, 1], F32, name="eps_t")
+        dummy = const.tile([P, 1], F32, name="dummy")
+        w_swap = const.tile([P, J, 2], F32, name="w_swap")
+        tab_a = const.tile([P, NT, D], F32, name="tab_a")
+        tab_b = const.tile([P, NT, D], F32, name="tab_b")
+
+        nc.vector.memset(xs[:].bitcast(I32), 0)
+        nc.vector.memset(ws[:].bitcast(I32), 0)
+        nc.gpsimd.memset(wrow[:], 0.0)
+        nc.gpsimd.memset(ones[:], 1.0)
+        nc.gpsimd.memset(eps_t[:], EPS)
+
+        nc.sync.dma_start(out=xc[:], in_=x_words.rearrange("g p n -> p g n"))
+        nc.sync.dma_start(out=wc[0][:], in_=wq_words[:, :, 0 : 2 * NB].rearrange("g p n -> p g n"))
+        for q in range(4):
+            nc.sync.dma_start(
+                out=xs[32 * q : 32 * q + 4, :, :].bitcast(I32),
+                in_=x_scales[:, 4 * q : 4 * q + 4, :].rearrange("g r n -> r g n").bitcast(I32),
+            )
+        for q in range(4):
+            nc.sync.dma_start(
+                out=ws[32 * q : 32 * q + 4, :, :].bitcast(I32),
+                in_=wq_scales[:, 4 * q : 4 * q + 4, :].rearrange("g r n -> r g n").bitcast(I32),
+            )
+        for n in range(1, NBK):
+            nc.sync.dma_start(
+                out=wc[n][:], in_=wq_words[:, :, 2 * NB * n : 2 * NB * (n + 1)].rearrange("g p n -> p g n")
+            )
+
+        nc.scalar.dma_start(out=wrow[0:1, 0:D], in_=q_norm_w.rearrange("(o d) -> o d", o=1))
+        nc.scalar.dma_start(out=cos_sb[:], in_=freqs_cos.rearrange("(i p) j -> p i j", p=P))
+        nc.scalar.dma_start(out=sin_sb[:], in_=freqs_sin.rearrange("(i p) j -> p i j", p=P))
+        nc.scalar.activation(out=dummy[:], in_=eps_t[:], func=AF.Sqrt)
+
+        w_ps = psum.tile([P, NB], F32, name="acc")
+        nc.tensor.matmul(out=w_ps[:, 0 : 2 * D], lhsT=ones[:], rhs=wrow[:], start=True, stop=True)
+        w_pair = w_ps[:, 0:D].rearrange("p (j e) -> p j e", e=2)
+        nc.vector.tensor_scalar(
+            out=w_swap[:, :, 0:1], in0=w_pair[:, :, 1:2], scalar1=-1.0, scalar2=None, op0=ALU.mult
+        )
+        nc.vector.tensor_copy(out=w_swap[:, :, 1:2], in_=w_pair[:, :, 0:1])
+        shape4 = [P, NT, J, 2]
+        nc.vector.tensor_tensor(
+            out=tab_a[:].rearrange("p i (j e) -> p i j e", e=2),
+            in0=cos_sb[:].rearrange("p i (j o) -> p i j o", o=1).to_broadcast(shape4),
+            in1=w_ps[:, 0:D].rearrange("p (o j e) -> p o j e", o=1, e=2).to_broadcast(shape4),
+            op=ALU.mult,
+        )
+        nc.vector.tensor_tensor(
+            out=tab_b[:].rearrange("p i (j e) -> p i j e", e=2),
+            in0=sin_sb[:].rearrange("p i (j o) -> p i j o", o=1).to_broadcast(shape4),
+            in1=w_swap[:].rearrange("p (o j) e -> p o j e", o=1).to_broadcast(shape4),
+            op=ALU.mult,
+        )
+
+        accs = {}
+        sds = {}
+        rstds = {}
+
+        def groups(i):
+            if i == 0:
+                return [(HB * n, HB) for n in range(NBK)]
+            return [(0, H)]
+
+        def stage_a(i):
+            ss = stat.tile([P, H], F32, name="ss")
+            sd = stat.tile([P, H], F32, name="sd")
+            rstd = stat.tile([P, H], F32, name="rstd")
+            sds[i] = sd
+            rstds[i] = rstd
+            for n in range(NBK):
+                acc = psum.tile([P, NB], F32, name="acc")
+                accs[(i, n)] = acc
+                for g in range(G):
+                    nc.tensor.matmul_mx(
+                        out=acc[:],
+                        lhsT=xc[:, g, 2 * P * i : 2 * P * (i + 1)].bitcast(FP4),
+                        lhsT_scale=xs[:, g, P * i : P * (i + 1)],
+                        rhs=wc[n][:, g, :].bitcast(FP4),
+                        rhs_scale=ws[:, g, NB * n : NB * (n + 1)],
+                        start=(g == 0),
+                        stop=(g == G - 1),
+                    )
+                for h in range(HB):
+                    junk = work.tile([P, D], F32, name="junk")
+                    c = HB * n + h
+                    nc.scalar.activation(
+                        out=junk[:], in_=acc[:, D * h : D * (h + 1)], func=AF.Square,
+                        scale=1.0 / math.sqrt(D), accum_out=ss[:, c : c + 1],
+                    )
+                for (c0, cn) in groups(i):
+                    if c0 + cn == HB * (n + 1):
+                        nc.scalar.activation(
+                            out=sd[:, c0 : c0 + cn], in_=ss[:, c0 : c0 + cn], func=AF.Sqrt,
+                            bias=eps_t[:, 0:1], scale=1.0,
+                        )
+
+        def recip(i, c0, cn):
+            nc.vector.reciprocal(out=rstds[i][:, c0 : c0 + cn], in_=sds[i][:, c0 : c0 + cn])
+
+        def bank(i, n):
+            acc = accs[(i, n)]
+            rstd = rstds[i]
+            m1 = work.tile([P, NB], F32, name="m1")
+            m2 = work.tile([P, NB], F32, name="m2")
+            y = work.tile([P, NB], F32, name="y")
+            late = (i * NBK + n) in Q_BANKS
+            if late:
+                s3 = [P, HB, D]
+                s4 = [P, HB, J, 2]
+                nc.vector.tensor_tensor(
+                    out=m1[:].rearrange("p (h d) -> p h d", h=HB),
+                    in0=acc[:].rearrange("p (h d) -> p h d", h=HB),
+                    in1=tab_a[:, i, :].rearrange("p (o d) -> p o d", o=1).to_broadcast(s3),
+                    op=ALU.mult,
+                )
+                nc.vector.tensor_tensor(
+                    out=m2[:].rearrange("p (h j e) -> p h j e", h=HB, e=2),
+                    in0=acc[:].rearrange("p (h j e) -> p h j e", h=HB, e=2)[:, :, :, ::-1],
+                    in1=tab_b[:, i, :].rearrange("p (o j e) -> p o j e", o=1, e=2).to_broadcast(s4),
+                    op=ALU.mult,
+                )
+                s = work.tile([P, NB], F32, name="s")
+                nc.gpsimd.tensor_tensor(out=s[:], in0=m1[:], in1=m2[:], op=ALU.add)
+                for h in range(HB):
+                    c = HB * n + h
+                    nc.scalar.activation(
+                        out=y[:, D * h : D * (h + 1)], in_=s[:, D * h : D * (h + 1)], func=AF.Copy,
+                        scale=rstd[:, c : c + 1],
+                    )
+            else:
+                for h in range(HB):
+                    c = HB * n + h
+                    cols = slice(D * h, D * (h + 1))
+                    nc.vector.scalar_tensor_tensor(
+                        out=m1[:, cols], in0=acc[:, cols], scalar=rstd[:, c : c + 1], in1=tab_a[:, i, :],
+                        op0=ALU.mult, op1=ALU.mult,
+                    )
+                    nc.vector.scalar_tensor_tensor(
+                        out=m2[:, cols].rearrange("p (j e) -> p j e", e=2),
+                        in0=acc[:, cols].rearrange("p (j e) -> p j e", e=2)[:, :, ::-1],
+                        scalar=rstd[:, c : c + 1],
+                        in1=tab_b[:, i, :].rearrange("p (j e) -> p j e", e=2),
+                        op0=ALU.mult, op1=ALU.mult,
+                    )
+                nc.gpsimd.tensor_tensor(out=y[:], in0=m1[:], in1=m2[:], op=ALU.add)
+            nc.sync.dma_start(out=out2[P * i : P * (i + 1), NB * n : NB * (n + 1)], in_=y[:])
+
+        stage_a(0)
+        for i in range(NT):
+            if i + 1 < NT:
+                stage_a(i + 1)
+            for n in range(NBK):
+                if i == 0:
+                    recip(0, HB * n, HB)
+                if n == NBK - 1 and i + 1 < NT:
+                    recip(i + 1, 0, H)
+                bank(i, n)

@@ -2,6 +2,7 @@ from contextlib import ExitStack
 import math
 
 import concourse.mybir as mybir
+from concourse.masks import make_identity
 
 T, C, H, D = 1024, 1024, 16, 128
 N = H * D
@@ -23,8 +24,17 @@ NB = 512
 NBK = N // NB
 HB = NB // D
 J = D // 2
+NBANKS = NT * NBK
 
-Q_BANKS = ()
+T_BANKS = (0, 4, 8, 12, 16, 20, 24, 28)
+Q_BANKS = (1, 5, 9, 13, 17, 21, 25)
+GROUPS = ((1, 3), (5, 3), (9, 3), (13, 3), (17, 3), (21, 3), (25, 3), (29, 1), (30, 1), (31, 1))
+V_ADDS = (30, 31)
+NA = 6
+LA = 5
+SC_T = 3
+SC_Q = 3
+SCALES_FIRST = False
 
 
 def tile_mla_pb_kernel(tc, x_words, x_scales, wq_words, wq_scales, q_norm_w, freqs_cos, freqs_sin, out):
@@ -33,9 +43,10 @@ def tile_mla_pb_kernel(tc, x_words, x_scales, wq_words, wq_scales, q_norm_w, fre
 
     with ExitStack() as ctx:
         const = ctx.enter_context(tc.tile_pool(name="const", bufs=1))
-        work = ctx.enter_context(tc.tile_pool(name="work", bufs=4))
-        stat = ctx.enter_context(tc.tile_pool(name="stat", bufs=3))
-        psum = ctx.enter_context(tc.psum_pool(name="psum", bufs=8))
+        work = ctx.enter_context(tc.tile_pool(name="work", bufs=5))
+        stat = ctx.enter_context(tc.tile_pool(name="stat", bufs=4))
+        psum = ctx.enter_context(tc.psum_pool(name="psum", bufs=NA))
+        psum2 = ctx.enter_context(tc.psum_pool(name="psum2", bufs=8 - NA))
         ctx.enter_context(tc.manual_schedule())
 
         xc = const.tile([P, G, 2 * T], U8, name="xc", align_bytes=64)
@@ -49,161 +60,202 @@ def tile_mla_pb_kernel(tc, x_words, x_scales, wq_words, wq_scales, q_norm_w, fre
         sin_sb = const.tile([P, NT, J], BF16, name="sin_sb")
         wrow = const.tile([P, 2 * D], BF16, name="wrow")
         ones = const.tile([P, P], BF16, name="ones")
+        ident = const.tile([P, P], F32, name="ident")
         eps_t = const.tile([P, 1], F32, name="eps_t")
         dummy = const.tile([P, 1], F32, name="dummy")
+        w_sb = const.tile([P, J, 2], F32, name="w_sb")
         w_swap = const.tile([P, J, 2], F32, name="w_swap")
         tab_a = const.tile([P, NT, D], F32, name="tab_a")
         tab_b = const.tile([P, NT, D], F32, name="tab_b")
 
         nc.vector.memset(xs[:].bitcast(I32), 0)
         nc.vector.memset(ws[:].bitcast(I32), 0)
+        nc.vector.memset(eps_t[:], EPS)
         nc.gpsimd.memset(wrow[:], 0.0)
+        nc.gpsimd.dma_start(out=wrow[0:1, 0:D], in_=q_norm_w.rearrange("(o d) -> o d", o=1))
         nc.gpsimd.memset(ones[:], 1.0)
-        nc.gpsimd.memset(eps_t[:], EPS)
+        nc.gpsimd.dma_start(out=cos_sb[:], in_=freqs_cos.rearrange("(i p) j -> p i j", p=P))
+        nc.gpsimd.dma_start(out=sin_sb[:], in_=freqs_sin.rearrange("(i p) j -> p i j", p=P))
+        make_identity(nc, ident[:])
 
-        nc.sync.dma_start(out=xc[:], in_=x_words.rearrange("g p n -> p g n"))
-        nc.sync.dma_start(out=wc[0][:], in_=wq_words[:, :, 0 : 2 * NB].rearrange("g p n -> p g n"))
-        for q in range(4):
-            nc.sync.dma_start(
-                out=xs[32 * q : 32 * q + 4, :, :].bitcast(I32),
-                in_=x_scales[:, 4 * q : 4 * q + 4, :].rearrange("g r n -> r g n").bitcast(I32),
-            )
-        for q in range(4):
-            nc.sync.dma_start(
-                out=ws[32 * q : 32 * q + 4, :, :].bitcast(I32),
-                in_=wq_scales[:, 4 * q : 4 * q + 4, :].rearrange("g r n -> r g n").bitcast(I32),
-            )
-        for n in range(1, NBK):
-            nc.sync.dma_start(
-                out=wc[n][:], in_=wq_words[:, :, 2 * NB * n : 2 * NB * (n + 1)].rearrange("g p n -> p g n")
-            )
+        def load_codes(first):
+            if first:
+                nc.sync.dma_start(out=xc[:], in_=x_words.rearrange("g p n -> p g n"))
+            for n in (range(0, 1) if first else range(1, NBK)):
+                nc.sync.dma_start(
+                    out=wc[n][:], in_=wq_words[:, :, 2 * NB * n : 2 * NB * (n + 1)].rearrange("g p n -> p g n")
+                )
 
-        nc.scalar.dma_start(out=wrow[0:1, 0:D], in_=q_norm_w.rearrange("(o d) -> o d", o=1))
-        nc.scalar.dma_start(out=cos_sb[:], in_=freqs_cos.rearrange("(i p) j -> p i j", p=P))
-        nc.scalar.dma_start(out=sin_sb[:], in_=freqs_sin.rearrange("(i p) j -> p i j", p=P))
-        nc.scalar.activation(out=dummy[:], in_=eps_t[:], func=AF.Sqrt)
+        if not SCALES_FIRST:
+            load_codes(True)
+        for (plane, src) in ((xs, x_scales), (ws, wq_scales)):
+            for q in range(4):
+                nc.sync.dma_start(
+                    out=plane[32 * q : 32 * q + 4, :, :].bitcast(I32),
+                    in_=src[:, 4 * q : 4 * q + 4, :].rearrange("g r n -> r g n").bitcast(I32),
+                )
+        if SCALES_FIRST:
+            load_codes(True)
+        load_codes(False)
 
-        w_ps = psum.tile([P, NB], F32, name="acc")
+        nc.scalar.activation(out=dummy[:], in_=eps_t[:], func=AF.Abs_reciprocal_sqrt)
+
+        w_ps = psum2.tile([P, NB], F32, name="sum_ps")
         nc.tensor.matmul(out=w_ps[:, 0 : 2 * D], lhsT=ones[:], rhs=wrow[:], start=True, stop=True)
         w_pair = w_ps[:, 0:D].rearrange("p (j e) -> p j e", e=2)
+        nc.vector.tensor_copy(out=w_sb[:], in_=w_pair)
         nc.vector.tensor_scalar(
             out=w_swap[:, :, 0:1], in0=w_pair[:, :, 1:2], scalar1=-1.0, scalar2=None, op0=ALU.mult
         )
         nc.vector.tensor_copy(out=w_swap[:, :, 1:2], in_=w_pair[:, :, 0:1])
-        shape4 = [P, NT, J, 2]
-        nc.vector.tensor_tensor(
-            out=tab_a[:].rearrange("p i (j e) -> p i j e", e=2),
-            in0=cos_sb[:].rearrange("p i (j o) -> p i j o", o=1).to_broadcast(shape4),
-            in1=w_ps[:, 0:D].rearrange("p (o j e) -> p o j e", o=1, e=2).to_broadcast(shape4),
-            op=ALU.mult,
-        )
-        nc.vector.tensor_tensor(
-            out=tab_b[:].rearrange("p i (j e) -> p i j e", e=2),
-            in0=sin_sb[:].rearrange("p i (j o) -> p i j o", o=1).to_broadcast(shape4),
-            in1=w_swap[:].rearrange("p (o j) e -> p o j e", o=1).to_broadcast(shape4),
-            op=ALU.mult,
-        )
+
+        def tables(eng, i0, i1):
+            shape4 = [P, i1 - i0, J, 2]
+            for (tab, trig, gain) in ((tab_a, cos_sb, w_sb), (tab_b, sin_sb, w_swap)):
+                eng.tensor_tensor(
+                    out=tab[:, i0:i1, :].rearrange("p i (j e) -> p i j e", e=2),
+                    in0=trig[:, i0:i1, :].rearrange("p i (j o) -> p i j o", o=1).to_broadcast(shape4),
+                    in1=gain[:].rearrange("p (o j) e -> p o j e", o=1).to_broadcast(shape4),
+                    op=ALU.mult,
+                )
+
+        tables(nc.vector, 0, 1)
+        tables(nc.gpsimd, 1, NT)
 
         accs = {}
-        sds = {}
+        sss = {}
         rstds = {}
+        sums = {}
+        runs = {}
+        run_of = {}
+        for (b0, cnt) in GROUPS:
+            for b in range(b0, b0 + cnt):
+                run_of[b] = (b0, cnt)
 
-        def groups(i):
-            if i == 0:
-                return [(HB * n, HB) for n in range(NBK)]
-            return [(0, H)]
-
-        def stage_a(i):
-            ss = stat.tile([P, H], F32, name="ss")
-            sd = stat.tile([P, H], F32, name="sd")
-            rstd = stat.tile([P, H], F32, name="rstd")
-            sds[i] = sd
-            rstds[i] = rstd
-            for n in range(NBK):
-                acc = psum.tile([P, NB], F32, name="acc")
-                accs[(i, n)] = acc
-                for g in range(G):
-                    nc.tensor.matmul_mx(
-                        out=acc[:],
-                        lhsT=xc[:, g, 2 * P * i : 2 * P * (i + 1)].bitcast(FP4),
-                        lhsT_scale=xs[:, g, P * i : P * (i + 1)],
-                        rhs=wc[n][:, g, :].bitcast(FP4),
-                        rhs_scale=ws[:, g, NB * n : NB * (n + 1)],
-                        start=(g == 0),
-                        stop=(g == G - 1),
-                    )
-                for h in range(HB):
-                    junk = work.tile([P, D], F32, name="junk")
-                    c = HB * n + h
-                    nc.scalar.activation(
-                        out=junk[:], in_=acc[:, D * h : D * (h + 1)], func=AF.Square,
-                        scale=1.0 / math.sqrt(D), accum_out=ss[:, c : c + 1],
-                    )
-                for (c0, cn) in groups(i):
-                    if c0 + cn == HB * (n + 1):
-                        nc.scalar.activation(
-                            out=sd[:, c0 : c0 + cn], in_=ss[:, c0 : c0 + cn], func=AF.Sqrt,
-                            bias=eps_t[:, 0:1], scale=1.0,
-                        )
-
-        def recip(i, c0, cn):
-            nc.vector.reciprocal(out=rstds[i][:, c0 : c0 + cn], in_=sds[i][:, c0 : c0 + cn])
-
-        def bank(i, n):
-            acc = accs[(i, n)]
-            rstd = rstds[i]
-            m1 = work.tile([P, NB], F32, name="m1")
-            m2 = work.tile([P, NB], F32, name="m2")
-            y = work.tile([P, NB], F32, name="y")
-            late = (i * NBK + n) in Q_BANKS
-            if late:
-                s3 = [P, HB, D]
-                s4 = [P, HB, J, 2]
-                nc.vector.tensor_tensor(
-                    out=m1[:].rearrange("p (h d) -> p h d", h=HB),
-                    in0=acc[:].rearrange("p (h d) -> p h d", h=HB),
-                    in1=tab_a[:, i, :].rearrange("p (o d) -> p o d", o=1).to_broadcast(s3),
-                    op=ALU.mult,
+        def mx(b):
+            i, n = divmod(b, NBK)
+            acc = psum.tile([P, NB], F32, name="acc")
+            accs[b] = acc
+            for g in range(G):
+                nc.tensor.matmul_mx(
+                    out=acc[:],
+                    lhsT=xc[:, g, 2 * P * i : 2 * P * (i + 1)].bitcast(FP4),
+                    lhsT_scale=xs[:, g, P * i : P * (i + 1)],
+                    rhs=wc[n][:, g, :].bitcast(FP4),
+                    rhs_scale=ws[:, g, NB * n : NB * (n + 1)],
+                    start=(g == 0),
+                    stop=(g == G - 1),
                 )
-                nc.vector.tensor_tensor(
-                    out=m2[:].rearrange("p (h j e) -> p h j e", h=HB, e=2),
-                    in0=acc[:].rearrange("p (h j e) -> p h j e", h=HB, e=2)[:, :, :, ::-1],
-                    in1=tab_b[:, i, :].rearrange("p (o j e) -> p o j e", o=1, e=2).to_broadcast(s4),
-                    op=ALU.mult,
+
+        def sumsq(b):
+            ss = stat.tile([P, HB], F32, name="ss")
+            rstd = stat.tile([P, HB], F32, name="rstd", bufs=12)
+            rstds[b] = rstd
+            for h in range(HB):
+                junk = work.tile([P, D], F32, name="junk")
+                nc.scalar.activation(
+                    out=junk[:], in_=accs[b][:, D * h : D * (h + 1)], func=AF.Square,
+                    scale=1.0 / math.sqrt(D), accum_out=ss[:, h : h + 1],
                 )
-                s = work.tile([P, NB], F32, name="s")
-                nc.gpsimd.tensor_tensor(out=s[:], in0=m1[:], in1=m2[:], op=ALU.add)
-                for h in range(HB):
-                    c = HB * n + h
-                    nc.scalar.activation(
-                        out=y[:, D * h : D * (h + 1)], in_=s[:, D * h : D * (h + 1)], func=AF.Copy,
-                        scale=rstd[:, c : c + 1],
-                    )
+            nc.scalar.activation(
+                out=rstd[:], in_=ss[:], func=AF.Abs_reciprocal_sqrt, bias=eps_t[:, 0:1], scale=1.0
+            )
+
+        def store(b0, cnt, y):
+            i, n = divmod(b0, NBK)
+            nc.sync.dma_start(out=out2[P * i : P * (i + 1), NB * n : NB * (n + cnt)], in_=y)
+
+        def wide(acc, i, m1, m2):
+            nc.vector.tensor_tensor(
+                out=m1.rearrange("p (h d) -> p h d", h=HB),
+                in0=acc[:].rearrange("p (h d) -> p h d", h=HB),
+                in1=tab_a[:, i, :].rearrange("p (o d) -> p o d", o=1).to_broadcast([P, HB, D]),
+                op=ALU.mult,
+            )
+            nc.vector.tensor_tensor(
+                out=m2.rearrange("p (h j e) -> p h j e", h=HB, e=2),
+                in0=acc[:].rearrange("p (h j e) -> p h j e", h=HB, e=2)[:, :, :, ::-1],
+                in1=tab_b[:, i, :].rearrange("p (o j e) -> p o j e", o=1, e=2).to_broadcast([P, HB, J, 2]),
+                op=ALU.mult,
+            )
+
+        def products(b):
+            i, n = divmod(b, NBK)
+            acc = accs[b]
+            if b in T_BANKS:
+                m1t = work.tile([P, NB], F32, name="m1t")
+                m2t = work.tile([P, NB], F32, name="m2t")
+                wide(acc, i, m1t[:], m2t[:])
+                sum_ps = psum2.tile([P, NB], F32, name="sum_ps")
+                nc.tensor.matmul(out=sum_ps[:], lhsT=ident[:], rhs=m1t[:], start=True, stop=False)
+                nc.tensor.matmul(out=sum_ps[:], lhsT=ident[:], rhs=m2t[:], start=False, stop=True)
+                sums[b] = sum_ps
+                return
+            b0, cnt = run_of[b]
+            if b == b0:
+                m1 = work.tile([P, 3 * NB], F32, name="m1")
+                m2 = work.tile([P, 3 * NB], F32, name="m2")
+                y = work.tile([P, 3 * NB], F32, name="y")
+                runs[b0] = (m1, m2, y)
+            m1, m2, y = runs[b0]
+            off = NB * (b - b0)
+            if b in Q_BANKS:
+                wide(acc, i, m1[:, off : off + NB], m2[:, off : off + NB])
             else:
+                rstd = rstds[b]
                 for h in range(HB):
-                    c = HB * n + h
-                    cols = slice(D * h, D * (h + 1))
+                    cols = slice(off + D * h, off + D * (h + 1))
+                    src = slice(D * h, D * (h + 1))
                     nc.vector.scalar_tensor_tensor(
-                        out=m1[:, cols], in0=acc[:, cols], scalar=rstd[:, c : c + 1], in1=tab_a[:, i, :],
+                        out=m1[:, cols], in0=acc[:, src], scalar=rstd[:, h : h + 1], in1=tab_a[:, i, :],
                         op0=ALU.mult, op1=ALU.mult,
                     )
                     nc.vector.scalar_tensor_tensor(
                         out=m2[:, cols].rearrange("p (j e) -> p j e", e=2),
-                        in0=acc[:, cols].rearrange("p (j e) -> p j e", e=2)[:, :, ::-1],
-                        scalar=rstd[:, c : c + 1],
+                        in0=acc[:, src].rearrange("p (j e) -> p j e", e=2)[:, :, ::-1],
+                        scalar=rstd[:, h : h + 1],
                         in1=tab_b[:, i, :].rearrange("p (j e) -> p j e", e=2),
                         op0=ALU.mult, op1=ALU.mult,
                     )
-                nc.gpsimd.tensor_tensor(out=y[:], in0=m1[:], in1=m2[:], op=ALU.add)
-            nc.sync.dma_start(out=out2[P * i : P * (i + 1), NB * n : NB * (n + 1)], in_=y[:])
+            if b == b0 + cnt - 1:
+                w = NB * cnt
+                eng = nc.vector if b0 in V_ADDS else nc.gpsimd
+                eng.tensor_tensor(out=y[:, 0:w], in0=m1[:, 0:w], in1=m2[:, 0:w], op=ALU.add)
+                if not any(bb in Q_BANKS for bb in range(b0, b0 + cnt)):
+                    store(b0, cnt, y[:, 0:w])
 
-        stage_a(0)
-        for i in range(NT):
-            if i + 1 < NT:
-                stage_a(i + 1)
-            for n in range(NBK):
-                if i == 0:
-                    recip(0, HB * n, HB)
-                if n == NBK - 1 and i + 1 < NT:
-                    recip(i + 1, 0, H)
-                bank(i, n)
+        def scale_t(b):
+            yt = work.tile([P, NB], F32, name="yt")
+            for h in range(HB):
+                nc.scalar.activation(
+                    out=yt[:, D * h : D * (h + 1)], in_=sums[b][:, D * h : D * (h + 1)], func=AF.Copy,
+                    scale=rstds[b][:, h : h + 1],
+                )
+            store(b, 1, yt[:])
+
+        def scale_q(b0, cnt):
+            y = runs[b0][2]
+            for b in range(b0, b0 + cnt):
+                if b in Q_BANKS:
+                    for h in range(HB):
+                        cols = slice(NB * (b - b0) + D * h, NB * (b - b0) + D * (h + 1))
+                        nc.scalar.activation(
+                            out=y[:, cols], in_=y[:, cols], func=AF.Copy, scale=rstds[b][:, h : h + 1]
+                        )
+            store(b0, cnt, y[:, 0 : NB * cnt])
+
+        for s in range(-LA, NBANKS + max(SC_T, SC_Q) + 1):
+            a = s + LA
+            if a < NBANKS:
+                mx(a)
+                if a > 0:
+                    sumsq(a)
+            if s - SC_T in T_BANKS:
+                scale_t(s - SC_T)
+            for (b0, cnt) in GROUPS:
+                if b0 + cnt - 1 == s - SC_Q and any(bb in Q_BANKS for bb in range(b0, b0 + cnt)):
+                    scale_q(b0, cnt)
+            if 0 <= s < NBANKS:
+                products(s)
+            if s == 0:
+                sumsq(0)

@@ -27,14 +27,16 @@ J = D // 2
 NBANKS = NT * NBK
 
 T_BANKS = (0, 4, 8, 12, 16, 20, 24, 28)
-Q_BANKS = (1, 5, 9, 13, 17, 21, 25)
-GROUPS = ((1, 3), (5, 3), (9, 3), (13, 3), (17, 3), (21, 3), (25, 3), (29, 1), (30, 1), (31, 1))
+Q_RUNS = ((1, 1), (5, 1), (9, 1), (13, 1), (17, 1), (21, 1), (25, 1))
+P_RUNS = ((2, 2), (6, 2), (10, 2), (14, 2), (18, 2), (22, 2), (26, 2), (29, 1), (30, 1), (31, 1))
 V_ADDS = (30, 31)
+P_MAX = 2
+Q_MAX = 1
 NA = 6
 LA = 5
 SC_T = 3
-SC_Q = 3
-SCALES_FIRST = False
+SC_Q = 2
+V_TILES = 4
 
 
 def tile_mla_pb_kernel(tc, x_words, x_scales, wq_words, wq_scales, q_norm_w, freqs_cos, freqs_sin, out):
@@ -63,10 +65,12 @@ def tile_mla_pb_kernel(tc, x_words, x_scales, wq_words, wq_scales, q_norm_w, fre
         ident = const.tile([P, P], F32, name="ident")
         eps_t = const.tile([P, 1], F32, name="eps_t")
         dummy = const.tile([P, 1], F32, name="dummy")
-        w_sb = const.tile([P, J, 2], F32, name="w_sb")
-        w_swap = const.tile([P, J, 2], F32, name="w_swap")
-        tab_a = const.tile([P, NT, D], F32, name="tab_a")
-        tab_b = const.tile([P, NT, D], F32, name="tab_b")
+        w_nat = const.tile([P, J, 2], F32, name="w_nat")
+        w_own = const.tile([P, 2, J], F32, name="w_own")
+        w_oth = const.tile([P, 2, J], F32, name="w_oth")
+        tab_a = const.tile([P, NT, J, 2], F32, name="tab_a")
+        tab_ad = const.tile([P, NT, 2, J], F32, name="tab_ad")
+        tab_bd = const.tile([P, NT, 2, J], F32, name="tab_bd")
 
         nc.vector.memset(xs[:].bitcast(I32), 0)
         nc.vector.memset(ws[:].bitcast(I32), 0)
@@ -74,63 +78,72 @@ def tile_mla_pb_kernel(tc, x_words, x_scales, wq_words, wq_scales, q_norm_w, fre
         nc.gpsimd.memset(wrow[:], 0.0)
         nc.gpsimd.dma_start(out=wrow[0:1, 0:D], in_=q_norm_w.rearrange("(o d) -> o d", o=1))
         nc.gpsimd.memset(ones[:], 1.0)
-        nc.gpsimd.dma_start(out=cos_sb[:], in_=freqs_cos.rearrange("(i p) j -> p i j", p=P))
-        nc.gpsimd.dma_start(out=sin_sb[:], in_=freqs_sin.rearrange("(i p) j -> p i j", p=P))
         make_identity(nc, ident[:])
 
-        def load_codes(first):
-            if first:
-                nc.sync.dma_start(out=xc[:], in_=x_words.rearrange("g p n -> p g n"))
-            for n in (range(0, 1) if first else range(1, NBK)):
-                nc.sync.dma_start(
-                    out=wc[n][:], in_=wq_words[:, :, 2 * NB * n : 2 * NB * (n + 1)].rearrange("g p n -> p g n")
-                )
-
-        if not SCALES_FIRST:
-            load_codes(True)
+        nc.sync.dma_start(out=cos_sb[:], in_=freqs_cos.rearrange("(i p) j -> p i j", p=P))
+        nc.sync.dma_start(out=sin_sb[:], in_=freqs_sin.rearrange("(i p) j -> p i j", p=P))
+        nc.sync.dma_start(out=xc[:], in_=x_words.rearrange("g p n -> p g n"))
+        nc.sync.dma_start(out=wc[0][:], in_=wq_words[:, :, 0 : 2 * NB].rearrange("g p n -> p g n"))
         for (plane, src) in ((xs, x_scales), (ws, wq_scales)):
             for q in range(4):
                 nc.sync.dma_start(
                     out=plane[32 * q : 32 * q + 4, :, :].bitcast(I32),
                     in_=src[:, 4 * q : 4 * q + 4, :].rearrange("g r n -> r g n").bitcast(I32),
                 )
-        if SCALES_FIRST:
-            load_codes(True)
-        load_codes(False)
+        for n in range(1, NBK):
+            nc.sync.dma_start(
+                out=wc[n][:], in_=wq_words[:, :, 2 * NB * n : 2 * NB * (n + 1)].rearrange("g p n -> p g n")
+            )
 
         nc.scalar.activation(out=dummy[:], in_=eps_t[:], func=AF.Abs_reciprocal_sqrt)
 
         w_ps = psum2.tile([P, NB], F32, name="sum_ps")
         nc.tensor.matmul(out=w_ps[:, 0 : 2 * D], lhsT=ones[:], rhs=wrow[:], start=True, stop=True)
-        w_pair = w_ps[:, 0:D].rearrange("p (j e) -> p j e", e=2)
-        nc.vector.tensor_copy(out=w_sb[:], in_=w_pair)
+        w_je = w_ps[:, 0:D].rearrange("p (j e) -> p j e", e=2)
+        w_ej = w_ps[:, 0:D].rearrange("p (j e) -> p e j", e=2)
+        nc.vector.tensor_copy(out=w_own[:], in_=w_ej)
         nc.vector.tensor_scalar(
-            out=w_swap[:, :, 0:1], in0=w_pair[:, :, 1:2], scalar1=-1.0, scalar2=None, op0=ALU.mult
+            out=w_oth[:, 0:1, :], in0=w_ej[:, 1:2, :], scalar1=-1.0, scalar2=None, op0=ALU.mult
         )
-        nc.vector.tensor_copy(out=w_swap[:, :, 1:2], in_=w_pair[:, :, 0:1])
+        nc.vector.tensor_copy(out=w_oth[:, 1:2, :], in_=w_ej[:, 0:1, :])
+        nc.vector.tensor_copy(out=w_nat[:], in_=w_je)
 
         def tables(eng, i0, i1):
-            shape4 = [P, i1 - i0, J, 2]
-            for (tab, trig, gain) in ((tab_a, cos_sb, w_sb), (tab_b, sin_sb, w_swap)):
-                eng.tensor_tensor(
-                    out=tab[:, i0:i1, :].rearrange("p i (j e) -> p i j e", e=2),
-                    in0=trig[:, i0:i1, :].rearrange("p i (j o) -> p i j o", o=1).to_broadcast(shape4),
-                    in1=gain[:].rearrange("p (o j) e -> p o j e", o=1).to_broadcast(shape4),
-                    op=ALU.mult,
-                )
+            ni = i1 - i0
+            eng.tensor_tensor(
+                out=tab_ad[:, i0:i1, :, :],
+                in0=cos_sb[:, i0:i1, :].rearrange("p i (o j) -> p i o j", o=1).to_broadcast([P, ni, 2, J]),
+                in1=w_own[:].rearrange("p (o e) j -> p o e j", o=1).to_broadcast([P, ni, 2, J]),
+                op=ALU.mult,
+            )
+            eng.tensor_tensor(
+                out=tab_bd[:, i0:i1, :, :],
+                in0=sin_sb[:, i0:i1, :].rearrange("p i (o j) -> p i o j", o=1).to_broadcast([P, ni, 2, J]),
+                in1=w_oth[:].rearrange("p (o e) j -> p o e j", o=1).to_broadcast([P, ni, 2, J]),
+                op=ALU.mult,
+            )
+            eng.tensor_tensor(
+                out=tab_a[:, i0:i1, :, :],
+                in0=cos_sb[:, i0:i1, :].rearrange("p i (j o) -> p i j o", o=1).to_broadcast([P, ni, J, 2]),
+                in1=w_nat[:].rearrange("p (o j) e -> p o j e", o=1).to_broadcast([P, ni, J, 2]),
+                op=ALU.mult,
+            )
 
         tables(nc.vector, 0, 1)
-        tables(nc.gpsimd, 1, NT)
+        if V_TILES > 1:
+            tables(nc.vector, 1, V_TILES)
+        if V_TILES < NT:
+            tables(nc.gpsimd, V_TILES, NT)
 
         accs = {}
-        sss = {}
         rstds = {}
         sums = {}
         runs = {}
         run_of = {}
-        for (b0, cnt) in GROUPS:
+        for (b0, cnt) in Q_RUNS + P_RUNS:
             for b in range(b0, b0 + cnt):
                 run_of[b] = (b0, cnt)
+        q_first = [b0 for (b0, cnt) in Q_RUNS]
 
         def mx(b):
             i, n = divmod(b, NBK)
@@ -165,84 +178,90 @@ def tile_mla_pb_kernel(tc, x_words, x_scales, wq_words, wq_scales, q_norm_w, fre
             i, n = divmod(b0, NBK)
             nc.sync.dma_start(out=out2[P * i : P * (i + 1), NB * n : NB * (n + cnt)], in_=y)
 
-        def wide(acc, i, m1, m2):
+        def wide(b, m1, m2):
+            i = b // NBK
+            acc_hej = accs[b][:].rearrange("p (h j e) -> p h e j", h=HB, e=2)
             nc.vector.tensor_tensor(
-                out=m1.rearrange("p (h d) -> p h d", h=HB),
-                in0=acc[:].rearrange("p (h d) -> p h d", h=HB),
-                in1=tab_a[:, i, :].rearrange("p (o d) -> p o d", o=1).to_broadcast([P, HB, D]),
+                out=m1, in0=acc_hej,
+                in1=tab_ad[:, i, :, :].rearrange("p (o e) j -> p o e j", o=1).to_broadcast([P, HB, 2, J]),
                 op=ALU.mult,
             )
-            nc.vector.tensor_tensor(
-                out=m2.rearrange("p (h j e) -> p h j e", h=HB, e=2),
-                in0=acc[:].rearrange("p (h j e) -> p h j e", h=HB, e=2)[:, :, :, ::-1],
-                in1=tab_b[:, i, :].rearrange("p (o j e) -> p o j e", o=1, e=2).to_broadcast([P, HB, J, 2]),
-                op=ALU.mult,
-            )
+            for e in range(2):
+                nc.vector.tensor_tensor(
+                    out=m2[:, :, e, :], in0=acc_hej[:, :, 1 - e, :],
+                    in1=tab_bd[:, i, e : e + 1, :].to_broadcast([P, HB, J]), op=ALU.mult,
+                )
 
         def products(b):
             i, n = divmod(b, NBK)
             acc = accs[b]
             if b in T_BANKS:
-                m1t = work.tile([P, NB], F32, name="m1t")
-                m2t = work.tile([P, NB], F32, name="m2t")
-                wide(acc, i, m1t[:], m2t[:])
+                m1t = work.tile([P, HB, 2, J], F32, name="m1t")
+                m2t = work.tile([P, HB, 2, J], F32, name="m2t")
+                wide(b, m1t[:], m2t[:])
                 sum_ps = psum2.tile([P, NB], F32, name="sum_ps")
-                nc.tensor.matmul(out=sum_ps[:], lhsT=ident[:], rhs=m1t[:], start=True, stop=False)
-                nc.tensor.matmul(out=sum_ps[:], lhsT=ident[:], rhs=m2t[:], start=False, stop=True)
+                nc.tensor.matmul(
+                    out=sum_ps[:], lhsT=ident[:], rhs=m1t[:].rearrange("p h e j -> p (h e j)"), start=True, stop=False
+                )
+                nc.tensor.matmul(
+                    out=sum_ps[:], lhsT=ident[:], rhs=m2t[:].rearrange("p h e j -> p (h e j)"), start=False, stop=True
+                )
                 sums[b] = sum_ps
                 return
             b0, cnt = run_of[b]
-            if b == b0:
-                m1 = work.tile([P, 3 * NB], F32, name="m1")
-                m2 = work.tile([P, 3 * NB], F32, name="m2")
-                y = work.tile([P, 3 * NB], F32, name="y")
-                runs[b0] = (m1, m2, y)
-            m1, m2, y = runs[b0]
-            off = NB * (b - b0)
-            if b in Q_BANKS:
-                wide(acc, i, m1[:, off : off + NB], m2[:, off : off + NB])
-            else:
-                rstd = rstds[b]
-                for h in range(HB):
-                    cols = slice(off + D * h, off + D * (h + 1))
-                    src = slice(D * h, D * (h + 1))
-                    nc.vector.scalar_tensor_tensor(
-                        out=m1[:, cols], in0=acc[:, src], scalar=rstd[:, h : h + 1], in1=tab_a[:, i, :],
-                        op0=ALU.mult, op1=ALU.mult,
+            nh = HB * cnt
+            h0 = HB * (b - b0)
+            if b0 in q_first:
+                if b == b0:
+                    m1q = work.tile([P, Q_MAX * HB, 2, J], F32, name="m1q")
+                    m2q = work.tile([P, Q_MAX * HB, 2, J], F32, name="m2q")
+                    runs[b0] = (m1q, m2q)
+                m1q, m2q = runs[b0]
+                wide(b, m1q[:, h0 : h0 + HB, :, :], m2q[:, h0 : h0 + HB, :, :])
+                if b == b0 + cnt - 1:
+                    sq = work.tile([P, Q_MAX * HB, 2, J], F32, name="sq")
+                    nc.gpsimd.tensor_tensor(
+                        out=sq[:, 0:nh, :, :], in0=m1q[:, 0:nh, :, :], in1=m2q[:, 0:nh, :, :], op=ALU.add
                     )
+                    sums[b0] = sq
+                return
+            if b == b0:
+                m1 = work.tile([P, P_MAX * HB, J, 2], F32, name="m1")
+                m2 = work.tile([P, P_MAX * HB, 2, J], F32, name="m2")
+                runs[b0] = (m1, m2)
+            m1, m2 = runs[b0]
+            rstd = rstds[b]
+            for h in range(HB):
+                acc_je = acc[:, D * h : D * (h + 1)].rearrange("p (j e) -> p j e", e=2)
+                nc.vector.scalar_tensor_tensor(
+                    out=m1[:, h0 + h, :, :], in0=acc_je, scalar=rstd[:, h : h + 1], in1=tab_a[:, i, :, :],
+                    op0=ALU.mult, op1=ALU.mult,
+                )
+                for e in range(2):
                     nc.vector.scalar_tensor_tensor(
-                        out=m2[:, cols].rearrange("p (j e) -> p j e", e=2),
-                        in0=acc[:, src].rearrange("p (j e) -> p j e", e=2)[:, :, ::-1],
-                        scalar=rstd[:, h : h + 1],
-                        in1=tab_b[:, i, :].rearrange("p (j e) -> p j e", e=2),
-                        op0=ALU.mult, op1=ALU.mult,
+                        out=m2[:, h0 + h, e, :], in0=acc_je[:, :, 1 - e], scalar=rstd[:, h : h + 1],
+                        in1=tab_bd[:, i, e, :], op0=ALU.mult, op1=ALU.mult,
                     )
             if b == b0 + cnt - 1:
-                w = NB * cnt
+                y = work.tile([P, P_MAX * HB, J, 2], F32, name="y")
                 eng = nc.vector if b0 in V_ADDS else nc.gpsimd
-                eng.tensor_tensor(out=y[:, 0:w], in0=m1[:, 0:w], in1=m2[:, 0:w], op=ALU.add)
-                if not any(bb in Q_BANKS for bb in range(b0, b0 + cnt)):
-                    store(b0, cnt, y[:, 0:w])
-
-        def scale_t(b):
-            yt = work.tile([P, NB], F32, name="yt")
-            for h in range(HB):
-                nc.scalar.activation(
-                    out=yt[:, D * h : D * (h + 1)], in_=sums[b][:, D * h : D * (h + 1)], func=AF.Copy,
-                    scale=rstds[b][:, h : h + 1],
+                eng.tensor_tensor(
+                    out=y[:, 0:nh, :, :], in0=m1[:, 0:nh, :, :],
+                    in1=m2[:, 0:nh, :, :].rearrange("p h e j -> p h j e"), op=ALU.add,
                 )
-            store(b, 1, yt[:])
+                store(b0, cnt, y[:, 0:nh, :, :].rearrange("p h j e -> p (h j e)"))
 
-        def scale_q(b0, cnt):
-            y = runs[b0][2]
+        def scale_late(b0, cnt):
+            yl = work.tile([P, Q_MAX * HB, J, 2], F32, name="yl")
             for b in range(b0, b0 + cnt):
-                if b in Q_BANKS:
-                    for h in range(HB):
-                        cols = slice(NB * (b - b0) + D * h, NB * (b - b0) + D * (h + 1))
-                        nc.scalar.activation(
-                            out=y[:, cols], in_=y[:, cols], func=AF.Copy, scale=rstds[b][:, h : h + 1]
-                        )
-            store(b0, cnt, y[:, 0 : NB * cnt])
+                for h in range(HB):
+                    hh = HB * (b - b0) + h
+                    if b0 in T_BANKS:
+                        src = sums[b0][:, D * h : D * (h + 1)].rearrange("p (e j) -> p j e", e=2)
+                    else:
+                        src = sums[b0][:, hh, :, :].rearrange("p e j -> p j e")
+                    nc.scalar.activation(out=yl[:, hh, :, :], in_=src, func=AF.Copy, scale=rstds[b][:, h : h + 1])
+            store(b0, cnt, yl[:, 0 : HB * cnt, :, :].rearrange("p h j e -> p (h j e)"))
 
         for s in range(-LA, NBANKS + max(SC_T, SC_Q) + 1):
             a = s + LA
@@ -251,10 +270,10 @@ def tile_mla_pb_kernel(tc, x_words, x_scales, wq_words, wq_scales, q_norm_w, fre
                 if a > 0:
                     sumsq(a)
             if s - SC_T in T_BANKS:
-                scale_t(s - SC_T)
-            for (b0, cnt) in GROUPS:
-                if b0 + cnt - 1 == s - SC_Q and any(bb in Q_BANKS for bb in range(b0, b0 + cnt)):
-                    scale_q(b0, cnt)
+                scale_late(s - SC_T, 1)
+            for (b0, cnt) in Q_RUNS:
+                if b0 + cnt - 1 == s - SC_Q:
+                    scale_late(b0, cnt)
             if 0 <= s < NBANKS:
                 products(s)
             if s == 0:

@@ -26,22 +26,24 @@ HB = NB // D
 J = D // 2
 NBANKS = NT * NBK
 
-T_BANKS = (0, 4, 8, 12, 16, 20, 24, 28)
-Q_RUNS = ((1, 1), (5, 1), (9, 1), (13, 1), (17, 1), (21, 1), (25, 1))
-P_RUNS = ((2, 2), (6, 2), (10, 2), (14, 2), (18, 2), (22, 2), (26, 2), (29, 1), (30, 1), (31, 1))
-V_ADDS = (30, 31)
-P_MAX = 2
-Q_MAX = 1
+T_BANKS = (0, 4, 12, 16, 24, 28)
+F_BANKS = ()
+RUNS = ((1, 3), (5, 3), (8, 4), (13, 3), (17, 3), (20, 4), (25, 3), (29, 1), (30, 1), (31, 1))
+V_ADDS = (31,)
+RUN_MAX = 4
 NA = 6
 LA = 5
 SC_T = 3
-SC_Q = 2
-V_TILES = 4
+FG = 1
+V_TILES = 2
+XA = 2
+JF = 64
 
 
 def tile_mla_pb_kernel(tc, x_words, x_scales, wq_words, wq_scales, q_norm_w, freqs_cos, freqs_sin, out):
     nc = tc.nc
     out2 = out.rearrange("b t h d -> (b t) (h d)")
+    out4 = out.rearrange("b t h (j e) -> (b t) h j e", e=2)
 
     with ExitStack() as ctx:
         const = ctx.enter_context(tc.tile_pool(name="const", bufs=1))
@@ -51,7 +53,8 @@ def tile_mla_pb_kernel(tc, x_words, x_scales, wq_words, wq_scales, q_norm_w, fre
         psum2 = ctx.enter_context(tc.psum_pool(name="psum2", bufs=8 - NA))
         ctx.enter_context(tc.manual_schedule())
 
-        xc = const.tile([P, G, 2 * T], U8, name="xc", align_bytes=64)
+        xca = const.tile([P, G, 2 * P * XA], U8, name="xca", align_bytes=64)
+        xcb = const.tile([P, G, 2 * P * (NT - XA)], U8, name="xcb", align_bytes=64)
         xs = const.tile([P, G, T], U8, name="xs", align_bytes=64)
         ws = const.tile([P, G, N], U8, name="ws", align_bytes=64)
         wc = []
@@ -80,20 +83,34 @@ def tile_mla_pb_kernel(tc, x_words, x_scales, wq_words, wq_scales, q_norm_w, fre
         nc.gpsimd.memset(ones[:], 1.0)
         make_identity(nc, ident[:])
 
-        nc.sync.dma_start(out=cos_sb[:], in_=freqs_cos.rearrange("(i p) j -> p i j", p=P))
-        nc.sync.dma_start(out=sin_sb[:], in_=freqs_sin.rearrange("(i p) j -> p i j", p=P))
-        nc.sync.dma_start(out=xc[:], in_=x_words.rearrange("g p n -> p g n"))
-        nc.sync.dma_start(out=wc[0][:], in_=wq_words[:, :, 0 : 2 * NB].rearrange("g p n -> p g n"))
-        for (plane, src) in ((xs, x_scales), (ws, wq_scales)):
+        def load_trig():
+            nc.sync.dma_start(out=cos_sb[:], in_=freqs_cos.rearrange("(i p) j -> p i j", p=P))
+            nc.sync.dma_start(out=sin_sb[:], in_=freqs_sin.rearrange("(i p) j -> p i j", p=P))
+
+        def load_first_codes():
+            nc.sync.dma_start(out=xca[:], in_=x_words[:, :, 0 : 2 * P * XA].rearrange("g p n -> p g n"))
+            nc.sync.dma_start(out=wc[0][:], in_=wq_words[:, :, 0 : 2 * NB].rearrange("g p n -> p g n"))
+
+        def load_scales(plane, src):
             for q in range(4):
                 nc.sync.dma_start(
                     out=plane[32 * q : 32 * q + 4, :, :].bitcast(I32),
                     in_=src[:, 4 * q : 4 * q + 4, :].rearrange("g r n -> r g n").bitcast(I32),
                 )
-        for n in range(1, NBK):
-            nc.sync.dma_start(
-                out=wc[n][:], in_=wq_words[:, :, 2 * NB * n : 2 * NB * (n + 1)].rearrange("g p n -> p g n")
-            )
+
+        for step in ("trig", "codes", "xs", "ws"):
+            if step == "trig":
+                load_trig()
+            elif step == "codes":
+                load_first_codes()
+            elif step == "xs":
+                load_scales(xs, x_scales)
+            else:
+                load_scales(ws, wq_scales)
+        nc.sync.dma_start(out=wc[1][:], in_=wq_words[:, :, 2 * NB : 4 * NB].rearrange("g p n -> p g n"))
+        nc.sync.dma_start(out=wc[2][:], in_=wq_words[:, :, 4 * NB : 6 * NB].rearrange("g p n -> p g n"))
+        nc.sync.dma_start(out=wc[3][:], in_=wq_words[:, :, 6 * NB : 8 * NB].rearrange("g p n -> p g n"))
+        nc.sync.dma_start(out=xcb[:], in_=x_words[:, :, 2 * P * XA : 2 * T].rearrange("g p n -> p g n"))
 
         nc.scalar.activation(out=dummy[:], in_=eps_t[:], func=AF.Abs_reciprocal_sqrt)
 
@@ -139,20 +156,24 @@ def tile_mla_pb_kernel(tc, x_words, x_scales, wq_words, wq_scales, q_norm_w, fre
         rstds = {}
         sums = {}
         runs = {}
+        qns = {}
         run_of = {}
-        for (b0, cnt) in Q_RUNS + P_RUNS:
+        for (b0, cnt) in RUNS:
             for b in range(b0, b0 + cnt):
                 run_of[b] = (b0, cnt)
-        q_first = [b0 for (b0, cnt) in Q_RUNS]
 
         def mx(b):
             i, n = divmod(b, NBK)
             acc = psum.tile([P, NB], F32, name="acc")
             accs[b] = acc
             for g in range(G):
+                if i < XA:
+                    codes = xca[:, g, 2 * P * i : 2 * P * (i + 1)]
+                else:
+                    codes = xcb[:, g, 2 * P * (i - XA) : 2 * P * (i - XA + 1)]
                 nc.tensor.matmul_mx(
                     out=acc[:],
-                    lhsT=xc[:, g, 2 * P * i : 2 * P * (i + 1)].bitcast(FP4),
+                    lhsT=codes.bitcast(FP4),
                     lhsT_scale=xs[:, g, P * i : P * (i + 1)],
                     rhs=wc[n][:, g, :].bitcast(FP4),
                     rhs_scale=ws[:, g, NB * n : NB * (n + 1)],
@@ -173,24 +194,71 @@ def tile_mla_pb_kernel(tc, x_words, x_scales, wq_words, wq_scales, q_norm_w, fre
             nc.scalar.activation(
                 out=rstd[:], in_=ss[:], func=AF.Abs_reciprocal_sqrt, bias=eps_t[:, 0:1], scale=1.0
             )
+            if b in F_BANKS:
+                qn = work.tile([P, HB, J, 2], F32, name="qn", bufs=2)
+                qns[b] = qn
+                for h in range(HB):
+                    nc.scalar.activation(
+                        out=qn[:, h, :, :], in_=accs[b][:, D * h : D * (h + 1)].rearrange("p (j e) -> p j e", e=2),
+                        func=AF.Copy, scale=rstd[:, h : h + 1],
+                    )
 
-        def store(b0, cnt, y):
+        def run_tiles(b):
+            b0, cnt = run_of[b]
+            if b0 not in runs:
+                m1 = work.tile([P, RUN_MAX * HB, J, 2], F32, name="m1")
+                m2 = work.tile([P, RUN_MAX * HB, 2, J], F32, name="m2")
+                runs[b0] = [m1, m2, 0]
+            return runs[b0]
+
+        def run_done(b):
+            b0, cnt = run_of[b]
+            run = runs[b0]
+            run[2] += 1
+            if run[2] < cnt:
+                return
+            m1, m2 = run[0], run[1]
+            nh = HB * cnt
             i, n = divmod(b0, NBK)
-            nc.sync.dma_start(out=out2[P * i : P * (i + 1), NB * n : NB * (n + cnt)], in_=y)
+            y = work.tile([P, RUN_MAX * HB, J, 2], F32, name="y")
+            if b0 in V_ADDS:
+                nc.vector.tensor_tensor(
+                    out=y[:, 0:nh, :, :], in0=m1[:, 0:nh, :, :],
+                    in1=m2[:, 0:nh, :, :].rearrange("p h e j -> p h j e"), op=ALU.add,
+                )
+                jf = J
+            else:
+                nc.gpsimd.tensor_tensor(
+                    out=y[:, 0:nh, 0:JF, :], in0=m1[:, 0:nh, 0:JF, :],
+                    in1=m2[:, 0:nh, :, 0:JF].rearrange("p h e j -> p h j e"), op=ALU.add,
+                )
+                jf = JF
+            if jf == J:
+                nc.sync.dma_start(
+                    out=out2[P * i : P * (i + 1), NB * n : NB * (n + cnt)],
+                    in_=y[:, 0:nh, :, :].rearrange("p h j e -> p (h j e)"),
+                )
+            else:
+                nc.sync.dma_start(
+                    out=out4[P * i : P * (i + 1), HB * n : HB * n + nh, 0:jf, :], in_=y[:, 0:nh, 0:jf, :]
+                )
 
-        def wide(b, m1, m2):
+        def products_g(b):
             i = b // NBK
-            acc_hej = accs[b][:].rearrange("p (h j e) -> p h e j", h=HB, e=2)
-            nc.vector.tensor_tensor(
-                out=m1, in0=acc_hej,
-                in1=tab_ad[:, i, :, :].rearrange("p (o e) j -> p o e j", o=1).to_broadcast([P, HB, 2, J]),
-                op=ALU.mult,
+            b0, cnt = run_of[b]
+            m1, m2 = run_tiles(b)[0:2]
+            h0 = HB * (b - b0)
+            qn = qns[b]
+            nc.gpsimd.tensor_tensor(
+                out=m1[:, h0 : h0 + HB, 0:JF, :], in0=qn[:, :, 0:JF, :],
+                in1=tab_a[:, i : i + 1, 0:JF, :].to_broadcast([P, HB, JF, 2]), op=ALU.mult,
             )
             for e in range(2):
-                nc.vector.tensor_tensor(
-                    out=m2[:, :, e, :], in0=acc_hej[:, :, 1 - e, :],
-                    in1=tab_bd[:, i, e : e + 1, :].to_broadcast([P, HB, J]), op=ALU.mult,
+                nc.gpsimd.tensor_tensor(
+                    out=m2[:, h0 : h0 + HB, e, 0:JF], in0=qn[:, :, 0:JF, 1 - e],
+                    in1=tab_bd[:, i, e : e + 1, 0:JF].to_broadcast([P, HB, JF]), op=ALU.mult,
                 )
+            run_done(b)
 
         def products(b):
             i, n = divmod(b, NBK)
@@ -198,7 +266,17 @@ def tile_mla_pb_kernel(tc, x_words, x_scales, wq_words, wq_scales, q_norm_w, fre
             if b in T_BANKS:
                 m1t = work.tile([P, HB, 2, J], F32, name="m1t")
                 m2t = work.tile([P, HB, 2, J], F32, name="m2t")
-                wide(b, m1t[:], m2t[:])
+                acc_hej = acc[:].rearrange("p (h j e) -> p h e j", h=HB, e=2)
+                nc.vector.tensor_tensor(
+                    out=m1t[:], in0=acc_hej,
+                    in1=tab_ad[:, i, :, :].rearrange("p (o e) j -> p o e j", o=1).to_broadcast([P, HB, 2, J]),
+                    op=ALU.mult,
+                )
+                for e in range(2):
+                    nc.vector.tensor_tensor(
+                        out=m2t[:, :, e, :], in0=acc_hej[:, :, 1 - e, :],
+                        in1=tab_bd[:, i, e : e + 1, :].to_broadcast([P, HB, J]), op=ALU.mult,
+                    )
                 sum_ps = psum2.tile([P, NB], F32, name="sum_ps")
                 nc.tensor.matmul(
                     out=sum_ps[:], lhsT=ident[:], rhs=m1t[:].rearrange("p h e j -> p (h e j)"), start=True, stop=False
@@ -209,27 +287,8 @@ def tile_mla_pb_kernel(tc, x_words, x_scales, wq_words, wq_scales, q_norm_w, fre
                 sums[b] = sum_ps
                 return
             b0, cnt = run_of[b]
-            nh = HB * cnt
+            m1, m2 = run_tiles(b)[0:2]
             h0 = HB * (b - b0)
-            if b0 in q_first:
-                if b == b0:
-                    m1q = work.tile([P, Q_MAX * HB, 2, J], F32, name="m1q")
-                    m2q = work.tile([P, Q_MAX * HB, 2, J], F32, name="m2q")
-                    runs[b0] = (m1q, m2q)
-                m1q, m2q = runs[b0]
-                wide(b, m1q[:, h0 : h0 + HB, :, :], m2q[:, h0 : h0 + HB, :, :])
-                if b == b0 + cnt - 1:
-                    sq = work.tile([P, Q_MAX * HB, 2, J], F32, name="sq")
-                    nc.gpsimd.tensor_tensor(
-                        out=sq[:, 0:nh, :, :], in0=m1q[:, 0:nh, :, :], in1=m2q[:, 0:nh, :, :], op=ALU.add
-                    )
-                    sums[b0] = sq
-                return
-            if b == b0:
-                m1 = work.tile([P, P_MAX * HB, J, 2], F32, name="m1")
-                m2 = work.tile([P, P_MAX * HB, 2, J], F32, name="m2")
-                runs[b0] = (m1, m2)
-            m1, m2 = runs[b0]
             rstd = rstds[b]
             for h in range(HB):
                 acc_je = acc[:, D * h : D * (h + 1)].rearrange("p (j e) -> p j e", e=2)
@@ -242,39 +301,31 @@ def tile_mla_pb_kernel(tc, x_words, x_scales, wq_words, wq_scales, q_norm_w, fre
                         out=m2[:, h0 + h, e, :], in0=acc_je[:, :, 1 - e], scalar=rstd[:, h : h + 1],
                         in1=tab_bd[:, i, e, :], op0=ALU.mult, op1=ALU.mult,
                     )
-            if b == b0 + cnt - 1:
-                y = work.tile([P, P_MAX * HB, J, 2], F32, name="y")
-                eng = nc.vector if b0 in V_ADDS else nc.gpsimd
-                eng.tensor_tensor(
-                    out=y[:, 0:nh, :, :], in0=m1[:, 0:nh, :, :],
-                    in1=m2[:, 0:nh, :, :].rearrange("p h e j -> p h j e"), op=ALU.add,
+            run_done(b)
+
+        def scale_t(b):
+            i, n = divmod(b, NBK)
+            yt = work.tile([P, HB, J, 2], F32, name="yt")
+            for h in range(HB):
+                nc.scalar.activation(
+                    out=yt[:, h, :, :], in_=sums[b][:, D * h : D * (h + 1)].rearrange("p (e j) -> p j e", e=2),
+                    func=AF.Copy, scale=rstds[b][:, h : h + 1],
                 )
-                store(b0, cnt, y[:, 0:nh, :, :].rearrange("p h j e -> p (h j e)"))
+            nc.sync.dma_start(
+                out=out2[P * i : P * (i + 1), NB * n : NB * (n + 1)], in_=yt[:].rearrange("p h j e -> p (h j e)")
+            )
 
-        def scale_late(b0, cnt):
-            yl = work.tile([P, Q_MAX * HB, J, 2], F32, name="yl")
-            for b in range(b0, b0 + cnt):
-                for h in range(HB):
-                    hh = HB * (b - b0) + h
-                    if b0 in T_BANKS:
-                        src = sums[b0][:, D * h : D * (h + 1)].rearrange("p (e j) -> p j e", e=2)
-                    else:
-                        src = sums[b0][:, hh, :, :].rearrange("p e j -> p j e")
-                    nc.scalar.activation(out=yl[:, hh, :, :], in_=src, func=AF.Copy, scale=rstds[b][:, h : h + 1])
-            store(b0, cnt, yl[:, 0 : HB * cnt, :, :].rearrange("p h j e -> p (h j e)"))
-
-        for s in range(-LA, NBANKS + max(SC_T, SC_Q) + 1):
+        for s in range(-LA, NBANKS + SC_T + 1):
             a = s + LA
             if a < NBANKS:
                 mx(a)
                 if a > 0:
                     sumsq(a)
+            if a - FG in F_BANKS:
+                products_g(a - FG)
             if s - SC_T in T_BANKS:
-                scale_late(s - SC_T, 1)
-            for (b0, cnt) in Q_RUNS:
-                if b0 + cnt - 1 == s - SC_Q:
-                    scale_late(b0, cnt)
-            if 0 <= s < NBANKS:
+                scale_t(s - SC_T)
+            if 0 <= s < NBANKS and s not in F_BANKS:
                 products(s)
             if s == 0:
                 sumsq(0)

@@ -26,24 +26,23 @@ HB = NB // D
 J = D // 2
 NBANKS = NT * NBK
 
-T_BANKS = (0, 4, 12, 16, 24, 28)
-F_BANKS = ()
-RUNS = ((1, 3), (5, 3), (8, 4), (13, 3), (17, 3), (20, 4), (25, 3), (29, 1), (30, 1), (31, 1))
-V_ADDS = (31,)
-RUN_MAX = 4
+T_BANKS = (0, 4, 12, 16, 20, 24, 28)
+Q_RUNS = ()
+P_RUNS = ((1, 3), (5, 3), (8, 4), (13, 3), (17, 3), (21, 3), (25, 3), (29, 1), (30, 1), (31, 1))
+V_FIRST = (0,)
+P_MAX = 4
+Q_MAX = 1
 NA = 6
 LA = 5
 SC_T = 3
-FG = 1
+SC_Q = 2
 V_TILES = 2
 XA = 2
-JF = 64
 
 
 def tile_mla_pb_kernel(tc, x_words, x_scales, wq_words, wq_scales, q_norm_w, freqs_cos, freqs_sin, out):
     nc = tc.nc
     out2 = out.rearrange("b t h d -> (b t) (h d)")
-    out4 = out.rearrange("b t h (j e) -> (b t) h j e", e=2)
 
     with ExitStack() as ctx:
         const = ctx.enter_context(tc.tile_pool(name="const", bufs=1))
@@ -55,8 +54,10 @@ def tile_mla_pb_kernel(tc, x_words, x_scales, wq_words, wq_scales, q_norm_w, fre
 
         xca = const.tile([P, G, 2 * P * XA], U8, name="xca", align_bytes=64)
         xcb = const.tile([P, G, 2 * P * (NT - XA)], U8, name="xcb", align_bytes=64)
-        xs = const.tile([P, G, T], U8, name="xs", align_bytes=64)
-        ws = const.tile([P, G, N], U8, name="ws", align_bytes=64)
+        xsa = const.tile([P, G, P * XA], U8, name="xsa", align_bytes=64)
+        xsb = const.tile([P, G, T - P * XA], U8, name="xsb", align_bytes=64)
+        wsa = const.tile([P, G, N // 2], U8, name="wsa", align_bytes=64)
+        wsb = const.tile([P, G, N // 2], U8, name="wsb", align_bytes=64)
         wc = []
         for n in range(NBK):
             wc_n = const.tile([P, G, 2 * NB], U8, name="wc%d" % n, align_bytes=64)
@@ -75,22 +76,18 @@ def tile_mla_pb_kernel(tc, x_words, x_scales, wq_words, wq_scales, q_norm_w, fre
         tab_ad = const.tile([P, NT, 2, J], F32, name="tab_ad")
         tab_bd = const.tile([P, NT, 2, J], F32, name="tab_bd")
 
-        nc.vector.memset(xs[:].bitcast(I32), 0)
-        nc.vector.memset(ws[:].bitcast(I32), 0)
+        for plane in (xsa, wsa, wsb, xsb):
+            nc.vector.memset(plane[:].bitcast(I32), 0)
         nc.vector.memset(eps_t[:], EPS)
         nc.gpsimd.memset(wrow[:], 0.0)
         nc.gpsimd.dma_start(out=wrow[0:1, 0:D], in_=q_norm_w.rearrange("(o d) -> o d", o=1))
         nc.gpsimd.memset(ones[:], 1.0)
         make_identity(nc, ident[:])
 
-        def load_trig():
-            nc.sync.dma_start(out=cos_sb[:], in_=freqs_cos.rearrange("(i p) j -> p i j", p=P))
-            nc.sync.dma_start(out=sin_sb[:], in_=freqs_sin.rearrange("(i p) j -> p i j", p=P))
-
-        def load_first_codes():
-            nc.sync.dma_start(out=xca[:], in_=x_words[:, :, 0 : 2 * P * XA].rearrange("g p n -> p g n"))
-            nc.sync.dma_start(out=wc[0][:], in_=wq_words[:, :, 0 : 2 * NB].rearrange("g p n -> p g n"))
-
+        nc.sync.dma_start(out=cos_sb[:], in_=freqs_cos.rearrange("(i p) j -> p i j", p=P))
+        nc.sync.dma_start(out=sin_sb[:], in_=freqs_sin.rearrange("(i p) j -> p i j", p=P))
+        nc.sync.dma_start(out=xca[:], in_=x_words[:, :, 0 : 2 * P * XA].rearrange("g p n -> p g n"))
+        nc.sync.dma_start(out=wc[0][:], in_=wq_words[:, :, 0 : 2 * NB].rearrange("g p n -> p g n"))
         def load_scales(plane, src):
             for q in range(4):
                 nc.sync.dma_start(
@@ -98,18 +95,18 @@ def tile_mla_pb_kernel(tc, x_words, x_scales, wq_words, wq_scales, q_norm_w, fre
                     in_=src[:, 4 * q : 4 * q + 4, :].rearrange("g r n -> r g n").bitcast(I32),
                 )
 
-        for step in ("trig", "codes", "xs", "ws"):
-            if step == "trig":
-                load_trig()
-            elif step == "codes":
-                load_first_codes()
-            elif step == "xs":
-                load_scales(xs, x_scales)
-            else:
-                load_scales(ws, wq_scales)
-        nc.sync.dma_start(out=wc[1][:], in_=wq_words[:, :, 2 * NB : 4 * NB].rearrange("g p n -> p g n"))
-        nc.sync.dma_start(out=wc[2][:], in_=wq_words[:, :, 4 * NB : 6 * NB].rearrange("g p n -> p g n"))
-        nc.sync.dma_start(out=wc[3][:], in_=wq_words[:, :, 6 * NB : 8 * NB].rearrange("g p n -> p g n"))
+        def load_w(n):
+            nc.sync.dma_start(
+                out=wc[n][:], in_=wq_words[:, :, 2 * NB * n : 2 * NB * (n + 1)].rearrange("g p n -> p g n")
+            )
+
+        load_scales(xsa, x_scales[:, :, 0 : P * XA])
+        load_scales(wsa, wq_scales[:, :, 0 : N // 2])
+        load_w(1)
+        load_w(2)
+        load_scales(wsb, wq_scales[:, :, N // 2 : N])
+        load_w(3)
+        load_scales(xsb, x_scales[:, :, P * XA : T])
         nc.sync.dma_start(out=xcb[:], in_=x_words[:, :, 2 * P * XA : 2 * T].rearrange("g p n -> p g n"))
 
         nc.scalar.activation(out=dummy[:], in_=eps_t[:], func=AF.Abs_reciprocal_sqrt)
@@ -147,20 +144,18 @@ def tile_mla_pb_kernel(tc, x_words, x_scales, wq_words, wq_scales, q_norm_w, fre
             )
 
         tables(nc.vector, 0, 1)
-        if V_TILES > 1:
-            tables(nc.vector, 1, V_TILES)
-        if V_TILES < NT:
-            tables(nc.gpsimd, V_TILES, NT)
+        tables(nc.vector, 1, V_TILES)
+        tables(nc.gpsimd, V_TILES, NT)
 
         accs = {}
         rstds = {}
         sums = {}
         runs = {}
-        qns = {}
         run_of = {}
-        for (b0, cnt) in RUNS:
+        for (b0, cnt) in Q_RUNS + P_RUNS:
             for b in range(b0, b0 + cnt):
                 run_of[b] = (b0, cnt)
+        q_first = [b0 for (b0, cnt) in Q_RUNS]
 
         def mx(b):
             i, n = divmod(b, NBK)
@@ -169,14 +164,17 @@ def tile_mla_pb_kernel(tc, x_words, x_scales, wq_words, wq_scales, q_norm_w, fre
             for g in range(G):
                 if i < XA:
                     codes = xca[:, g, 2 * P * i : 2 * P * (i + 1)]
+                    x_plane = xsa[:, g, P * i : P * (i + 1)]
                 else:
                     codes = xcb[:, g, 2 * P * (i - XA) : 2 * P * (i - XA + 1)]
+                    x_plane = xsb[:, g, P * (i - XA) : P * (i - XA + 1)]
+                w_plane = (wsa, wsb)[n // 2][:, g, NB * (n % 2) : NB * (n % 2 + 1)]
                 nc.tensor.matmul_mx(
                     out=acc[:],
                     lhsT=codes.bitcast(FP4),
-                    lhsT_scale=xs[:, g, P * i : P * (i + 1)],
+                    lhsT_scale=x_plane,
                     rhs=wc[n][:, g, :].bitcast(FP4),
-                    rhs_scale=ws[:, g, NB * n : NB * (n + 1)],
+                    rhs_scale=w_plane,
                     start=(g == 0),
                     stop=(g == G - 1),
                 )
@@ -194,71 +192,33 @@ def tile_mla_pb_kernel(tc, x_words, x_scales, wq_words, wq_scales, q_norm_w, fre
             nc.scalar.activation(
                 out=rstd[:], in_=ss[:], func=AF.Abs_reciprocal_sqrt, bias=eps_t[:, 0:1], scale=1.0
             )
-            if b in F_BANKS:
-                qn = work.tile([P, HB, J, 2], F32, name="qn", bufs=2)
-                qns[b] = qn
-                for h in range(HB):
-                    nc.scalar.activation(
-                        out=qn[:, h, :, :], in_=accs[b][:, D * h : D * (h + 1)].rearrange("p (j e) -> p j e", e=2),
-                        func=AF.Copy, scale=rstd[:, h : h + 1],
-                    )
 
-        def run_tiles(b):
-            b0, cnt = run_of[b]
-            if b0 not in runs:
-                m1 = work.tile([P, RUN_MAX * HB, J, 2], F32, name="m1")
-                m2 = work.tile([P, RUN_MAX * HB, 2, J], F32, name="m2")
-                runs[b0] = [m1, m2, 0]
-            return runs[b0]
-
-        def run_done(b):
-            b0, cnt = run_of[b]
-            run = runs[b0]
-            run[2] += 1
-            if run[2] < cnt:
-                return
-            m1, m2 = run[0], run[1]
-            nh = HB * cnt
+        def store(b0, h0, nh, y):
             i, n = divmod(b0, NBK)
-            y = work.tile([P, RUN_MAX * HB, J, 2], F32, name="y")
-            if b0 in V_ADDS:
-                nc.vector.tensor_tensor(
-                    out=y[:, 0:nh, :, :], in0=m1[:, 0:nh, :, :],
-                    in1=m2[:, 0:nh, :, :].rearrange("p h e j -> p h j e"), op=ALU.add,
-                )
-                jf = J
-            else:
-                nc.gpsimd.tensor_tensor(
-                    out=y[:, 0:nh, 0:JF, :], in0=m1[:, 0:nh, 0:JF, :],
-                    in1=m2[:, 0:nh, :, 0:JF].rearrange("p h e j -> p h j e"), op=ALU.add,
-                )
-                jf = JF
-            if jf == J:
-                nc.sync.dma_start(
-                    out=out2[P * i : P * (i + 1), NB * n : NB * (n + cnt)],
-                    in_=y[:, 0:nh, :, :].rearrange("p h j e -> p (h j e)"),
-                )
-            else:
-                nc.sync.dma_start(
-                    out=out4[P * i : P * (i + 1), HB * n : HB * n + nh, 0:jf, :], in_=y[:, 0:nh, 0:jf, :]
-                )
+            c0 = NB * n + D * h0
+            nc.sync.dma_start(out=out2[P * i : P * (i + 1), c0 : c0 + D * nh], in_=y.rearrange("p h j e -> p (h j e)"))
 
-        def products_g(b):
+        def wide(b, m1, m2):
             i = b // NBK
-            b0, cnt = run_of[b]
-            m1, m2 = run_tiles(b)[0:2]
-            h0 = HB * (b - b0)
-            qn = qns[b]
-            nc.gpsimd.tensor_tensor(
-                out=m1[:, h0 : h0 + HB, 0:JF, :], in0=qn[:, :, 0:JF, :],
-                in1=tab_a[:, i : i + 1, 0:JF, :].to_broadcast([P, HB, JF, 2]), op=ALU.mult,
+            acc_hej = accs[b][:].rearrange("p (h j e) -> p h e j", h=HB, e=2)
+            nc.vector.tensor_tensor(
+                out=m1, in0=acc_hej,
+                in1=tab_ad[:, i, :, :].rearrange("p (o e) j -> p o e j", o=1).to_broadcast([P, HB, 2, J]),
+                op=ALU.mult,
             )
             for e in range(2):
-                nc.gpsimd.tensor_tensor(
-                    out=m2[:, h0 : h0 + HB, e, 0:JF], in0=qn[:, :, 0:JF, 1 - e],
-                    in1=tab_bd[:, i, e : e + 1, 0:JF].to_broadcast([P, HB, JF]), op=ALU.mult,
+                nc.vector.tensor_tensor(
+                    out=m2[:, :, e, :], in0=acc_hej[:, :, 1 - e, :],
+                    in1=tab_bd[:, i, e : e + 1, :].to_broadcast([P, HB, J]), op=ALU.mult,
                 )
-            run_done(b)
+
+        def add_heads(eng, b0, m1, m2, h0, nh):
+            y = work.tile([P, P_MAX * HB, J, 2], F32, name="y")
+            eng.tensor_tensor(
+                out=y[:, 0:nh, :, :], in0=m1[:, h0 : h0 + nh, :, :],
+                in1=m2[:, h0 : h0 + nh, :, :].rearrange("p h e j -> p h j e"), op=ALU.add,
+            )
+            store(b0, h0, nh, y[:, 0:nh, :, :])
 
         def products(b):
             i, n = divmod(b, NBK)
@@ -266,17 +226,7 @@ def tile_mla_pb_kernel(tc, x_words, x_scales, wq_words, wq_scales, q_norm_w, fre
             if b in T_BANKS:
                 m1t = work.tile([P, HB, 2, J], F32, name="m1t")
                 m2t = work.tile([P, HB, 2, J], F32, name="m2t")
-                acc_hej = acc[:].rearrange("p (h j e) -> p h e j", h=HB, e=2)
-                nc.vector.tensor_tensor(
-                    out=m1t[:], in0=acc_hej,
-                    in1=tab_ad[:, i, :, :].rearrange("p (o e) j -> p o e j", o=1).to_broadcast([P, HB, 2, J]),
-                    op=ALU.mult,
-                )
-                for e in range(2):
-                    nc.vector.tensor_tensor(
-                        out=m2t[:, :, e, :], in0=acc_hej[:, :, 1 - e, :],
-                        in1=tab_bd[:, i, e : e + 1, :].to_broadcast([P, HB, J]), op=ALU.mult,
-                    )
+                wide(b, m1t[:], m2t[:])
                 sum_ps = psum2.tile([P, NB], F32, name="sum_ps")
                 nc.tensor.matmul(
                     out=sum_ps[:], lhsT=ident[:], rhs=m1t[:].rearrange("p h e j -> p (h e j)"), start=True, stop=False
@@ -287,9 +237,29 @@ def tile_mla_pb_kernel(tc, x_words, x_scales, wq_words, wq_scales, q_norm_w, fre
                 sums[b] = sum_ps
                 return
             b0, cnt = run_of[b]
-            m1, m2 = run_tiles(b)[0:2]
+            nh = HB * cnt
             h0 = HB * (b - b0)
+            if b0 in q_first:
+                if b == b0:
+                    m1q = work.tile([P, Q_MAX * HB, 2, J], F32, name="m1q")
+                    m2q = work.tile([P, Q_MAX * HB, 2, J], F32, name="m2q")
+                    runs[b0] = (m1q, m2q)
+                m1q, m2q = runs[b0]
+                wide(b, m1q[:, h0 : h0 + HB, :, :], m2q[:, h0 : h0 + HB, :, :])
+                if b == b0 + cnt - 1:
+                    sq = work.tile([P, Q_MAX * HB, 2, J], F32, name="sq")
+                    nc.gpsimd.tensor_tensor(
+                        out=sq[:, 0:nh, :, :], in0=m1q[:, 0:nh, :, :], in1=m2q[:, 0:nh, :, :], op=ALU.add
+                    )
+                    sums[b0] = sq
+                return
+            if b == b0:
+                m1 = work.tile([P, P_MAX * HB, J, 2], F32, name="m1")
+                m2 = work.tile([P, P_MAX * HB, 2, J], F32, name="m2")
+                runs[b0] = (m1, m2)
+            m1, m2 = runs[b0]
             rstd = rstds[b]
+            last = b == NBANKS - 1
             for h in range(HB):
                 acc_je = acc[:, D * h : D * (h + 1)].rearrange("p (j e) -> p j e", e=2)
                 nc.vector.scalar_tensor_tensor(
@@ -301,31 +271,37 @@ def tile_mla_pb_kernel(tc, x_words, x_scales, wq_words, wq_scales, q_norm_w, fre
                         out=m2[:, h0 + h, e, :], in0=acc_je[:, :, 1 - e], scalar=rstd[:, h : h + 1],
                         in1=tab_bd[:, i, e, :], op0=ALU.mult, op1=ALU.mult,
                     )
-            run_done(b)
+                if last and h == 0 - 1:
+                    add_heads(nc.gpsimd, b0, m1, m2, 0, 0)
+            if last:
+                add_heads(nc.vector, b0, m1, m2, 0, HB - 0)
+            elif b == b0 + cnt - 1:
+                add_heads(nc.gpsimd, b0, m1, m2, 0, nh)
 
-        def scale_t(b):
-            i, n = divmod(b, NBK)
-            yt = work.tile([P, HB, J, 2], F32, name="yt")
-            for h in range(HB):
-                nc.scalar.activation(
-                    out=yt[:, h, :, :], in_=sums[b][:, D * h : D * (h + 1)].rearrange("p (e j) -> p j e", e=2),
-                    func=AF.Copy, scale=rstds[b][:, h : h + 1],
-                )
-            nc.sync.dma_start(
-                out=out2[P * i : P * (i + 1), NB * n : NB * (n + 1)], in_=yt[:].rearrange("p h j e -> p (h j e)")
-            )
+        def scale_late(b0, cnt):
+            yl = work.tile([P, Q_MAX * HB, J, 2], F32, name="yl")
+            for b in range(b0, b0 + cnt):
+                for h in range(HB):
+                    hh = HB * (b - b0) + h
+                    if b0 in T_BANKS:
+                        src = sums[b0][:, D * h : D * (h + 1)].rearrange("p (e j) -> p j e", e=2)
+                    else:
+                        src = sums[b0][:, hh, :, :].rearrange("p e j -> p j e")
+                    nc.scalar.activation(out=yl[:, hh, :, :], in_=src, func=AF.Copy, scale=rstds[b][:, h : h + 1])
+            store(b0, 0, HB * cnt, yl[:, 0 : HB * cnt, :, :])
 
-        for s in range(-LA, NBANKS + SC_T + 1):
+        for s in range(-LA, NBANKS + max(SC_T, SC_Q) + 1):
             a = s + LA
             if a < NBANKS:
                 mx(a)
-                if a > 0:
+                if a not in V_FIRST:
                     sumsq(a)
-            if a - FG in F_BANKS:
-                products_g(a - FG)
             if s - SC_T in T_BANKS:
-                scale_t(s - SC_T)
-            if 0 <= s < NBANKS and s not in F_BANKS:
+                scale_late(s - SC_T, 1)
+            for (b0, cnt) in Q_RUNS:
+                if b0 + cnt - 1 == s - SC_Q:
+                    scale_late(b0, cnt)
+            if 0 <= s < NBANKS:
                 products(s)
-            if s == 0:
-                sumsq(0)
+                if s in V_FIRST:
+                    sumsq(s)

@@ -27,15 +27,12 @@ J = D // 2
 NBANKS = NT * NBK
 
 T_BANKS = (0, 4, 12, 16, 20, 24, 28)
-Q_RUNS = ()
 P_RUNS = ((1, 3), (5, 3), (8, 4), (13, 3), (17, 3), (21, 3), (25, 3), (29, 1), (30, 1), (31, 1))
 V_FIRST = (0,)
 P_MAX = 4
-Q_MAX = 1
 NA = 6
 LA = 5
 SC_T = 3
-SC_Q = 2
 V_TILES = 2
 XA = 2
 
@@ -62,19 +59,14 @@ def tile_mla_pb_kernel(tc, x_words, x_scales, wq_words, wq_scales, q_norm_w, fre
         for n in range(NBK):
             wc_n = const.tile([P, G, 2 * NB], U8, name="wc%d" % n, align_bytes=64)
             wc.append(wc_n)
-        cos_sb = const.tile([P, NT, J], BF16, name="cos_sb")
-        sin_sb = const.tile([P, NT, J], BF16, name="sin_sb")
+        trig = const.tile([P, NT, 2, J], BF16, name="trig")
         wrow = const.tile([P, 2 * D], BF16, name="wrow")
         ones = const.tile([P, P], BF16, name="ones")
         ident = const.tile([P, P], F32, name="ident")
         eps_t = const.tile([P, 1], F32, name="eps_t")
         dummy = const.tile([P, 1], F32, name="dummy")
-        w_nat = const.tile([P, J, 2], F32, name="w_nat")
-        w_own = const.tile([P, 2, J], F32, name="w_own")
-        w_oth = const.tile([P, 2, J], F32, name="w_oth")
-        tab_a = const.tile([P, NT, J, 2], F32, name="tab_a")
-        tab_ad = const.tile([P, NT, 2, J], F32, name="tab_ad")
-        tab_bd = const.tile([P, NT, 2, J], F32, name="tab_bd")
+        w2 = const.tile([P, 2, J, 2], F32, name="w2")
+        tab = const.tile([P, NT, 2, D], F32, name="tab")
 
         for plane in (xsa, wsa, wsb, xsb):
             nc.vector.memset(plane[:].bitcast(I32), 0)
@@ -84,10 +76,11 @@ def tile_mla_pb_kernel(tc, x_words, x_scales, wq_words, wq_scales, q_norm_w, fre
         nc.gpsimd.memset(ones[:], 1.0)
         make_identity(nc, ident[:])
 
-        nc.sync.dma_start(out=cos_sb[:], in_=freqs_cos.rearrange("(i p) j -> p i j", p=P))
-        nc.sync.dma_start(out=sin_sb[:], in_=freqs_sin.rearrange("(i p) j -> p i j", p=P))
+        nc.sync.dma_start(out=trig[:, :, 0, :], in_=freqs_cos.rearrange("(i p) j -> p i j", p=P))
+        nc.sync.dma_start(out=trig[:, :, 1, :], in_=freqs_sin.rearrange("(i p) j -> p i j", p=P))
         nc.sync.dma_start(out=xca[:], in_=x_words[:, :, 0 : 2 * P * XA].rearrange("g p n -> p g n"))
         nc.sync.dma_start(out=wc[0][:], in_=wq_words[:, :, 0 : 2 * NB].rearrange("g p n -> p g n"))
+
         def load_scales(plane, src):
             for q in range(4):
                 nc.sync.dma_start(
@@ -114,32 +107,18 @@ def tile_mla_pb_kernel(tc, x_words, x_scales, wq_words, wq_scales, q_norm_w, fre
         w_ps = psum2.tile([P, NB], F32, name="sum_ps")
         nc.tensor.matmul(out=w_ps[:, 0 : 2 * D], lhsT=ones[:], rhs=wrow[:], start=True, stop=True)
         w_je = w_ps[:, 0:D].rearrange("p (j e) -> p j e", e=2)
-        w_ej = w_ps[:, 0:D].rearrange("p (j e) -> p e j", e=2)
-        nc.vector.tensor_copy(out=w_own[:], in_=w_ej)
+        nc.vector.tensor_copy(out=w2[:, 0, :, :], in_=w_je)
+        nc.vector.tensor_copy(out=w2[:, 1, :, 0:1], in_=w_je[:, :, 0:1])
         nc.vector.tensor_scalar(
-            out=w_oth[:, 0:1, :], in0=w_ej[:, 1:2, :], scalar1=-1.0, scalar2=None, op0=ALU.mult
+            out=w2[:, 1, :, 1:2], in0=w_je[:, :, 1:2], scalar1=-1.0, scalar2=None, op0=ALU.mult
         )
-        nc.vector.tensor_copy(out=w_oth[:, 1:2, :], in_=w_ej[:, 0:1, :])
-        nc.vector.tensor_copy(out=w_nat[:], in_=w_je)
 
         def tables(eng, i0, i1):
             ni = i1 - i0
             eng.tensor_tensor(
-                out=tab_ad[:, i0:i1, :, :],
-                in0=cos_sb[:, i0:i1, :].rearrange("p i (o j) -> p i o j", o=1).to_broadcast([P, ni, 2, J]),
-                in1=w_own[:].rearrange("p (o e) j -> p o e j", o=1).to_broadcast([P, ni, 2, J]),
-                op=ALU.mult,
-            )
-            eng.tensor_tensor(
-                out=tab_bd[:, i0:i1, :, :],
-                in0=sin_sb[:, i0:i1, :].rearrange("p i (o j) -> p i o j", o=1).to_broadcast([P, ni, 2, J]),
-                in1=w_oth[:].rearrange("p (o e) j -> p o e j", o=1).to_broadcast([P, ni, 2, J]),
-                op=ALU.mult,
-            )
-            eng.tensor_tensor(
-                out=tab_a[:, i0:i1, :, :],
-                in0=cos_sb[:, i0:i1, :].rearrange("p i (j o) -> p i j o", o=1).to_broadcast([P, ni, J, 2]),
-                in1=w_nat[:].rearrange("p (o j) e -> p o j e", o=1).to_broadcast([P, ni, J, 2]),
+                out=tab[:, i0:i1, :, :].rearrange("p i r (j e) -> p i (r j) e", e=2),
+                in0=trig[:, i0:i1, :, :].rearrange("p i r (j o) -> p i (r j) o", o=1).to_broadcast([P, ni, 2 * J, 2]),
+                in1=w2[:].rearrange("p (o r) j e -> p o (r j) e", o=1).to_broadcast([P, ni, 2 * J, 2]),
                 op=ALU.mult,
             )
 
@@ -152,10 +131,9 @@ def tile_mla_pb_kernel(tc, x_words, x_scales, wq_words, wq_scales, q_norm_w, fre
         sums = {}
         runs = {}
         run_of = {}
-        for (b0, cnt) in Q_RUNS + P_RUNS:
+        for (b0, cnt) in P_RUNS:
             for b in range(b0, b0 + cnt):
                 run_of[b] = (b0, cnt)
-        q_first = [b0 for (b0, cnt) in Q_RUNS]
 
         def mx(b):
             i, n = divmod(b, NBK)
@@ -193,114 +171,80 @@ def tile_mla_pb_kernel(tc, x_words, x_scales, wq_words, wq_scales, q_norm_w, fre
                 out=rstd[:], in_=ss[:], func=AF.Abs_reciprocal_sqrt, bias=eps_t[:, 0:1], scale=1.0
             )
 
-        def store(b0, h0, nh, y):
+        def store(b0, nh, y):
             i, n = divmod(b0, NBK)
-            c0 = NB * n + D * h0
+            c0 = NB * n
             nc.sync.dma_start(out=out2[P * i : P * (i + 1), c0 : c0 + D * nh], in_=y.rearrange("p h j e -> p (h j e)"))
 
-        def wide(b, m1, m2):
-            i = b // NBK
-            acc_hej = accs[b][:].rearrange("p (h j e) -> p h e j", h=HB, e=2)
-            nc.vector.tensor_tensor(
-                out=m1, in0=acc_hej,
-                in1=tab_ad[:, i, :, :].rearrange("p (o e) j -> p o e j", o=1).to_broadcast([P, HB, 2, J]),
-                op=ALU.mult,
-            )
-            for e in range(2):
-                nc.vector.tensor_tensor(
-                    out=m2[:, :, e, :], in0=acc_hej[:, :, 1 - e, :],
-                    in1=tab_bd[:, i, e : e + 1, :].to_broadcast([P, HB, J]), op=ALU.mult,
-                )
-
-        def add_heads(eng, b0, m1, m2, h0, nh):
+        def add_heads(eng, b0, m, nh):
             y = work.tile([P, P_MAX * HB, J, 2], F32, name="y")
             eng.tensor_tensor(
-                out=y[:, 0:nh, :, :], in0=m1[:, h0 : h0 + nh, :, :],
-                in1=m2[:, h0 : h0 + nh, :, :].rearrange("p h e j -> p h j e"), op=ALU.add,
+                out=y[:, 0:nh, :, :],
+                in0=m[:, 0:nh, 0, :].rearrange("p h (j e) -> p h j e", e=2),
+                in1=m[:, 0:nh, 1, :].rearrange("p h (j e) -> p h j e", e=2)[:, :, :, ::-1],
+                op=ALU.add,
             )
-            store(b0, h0, nh, y[:, 0:nh, :, :])
+            store(b0, nh, y[:, 0:nh, :, :])
 
         def products(b):
             i, n = divmod(b, NBK)
             acc = accs[b]
             if b in T_BANKS:
-                m1t = work.tile([P, HB, 2, J], F32, name="m1t")
-                m2t = work.tile([P, HB, 2, J], F32, name="m2t")
-                wide(b, m1t[:], m2t[:])
+                m1t = work.tile([P, HB, J, 2], F32, name="m1t")
+                m2t = work.tile([P, HB, J, 2], F32, name="m2t")
+                acc_hje = acc[:].rearrange("p (h j e) -> p h j e", h=HB, e=2)
+                tab_je = tab[:, i, :, :].rearrange("p r (o j e) -> p r o j e", o=1, e=2)
+                nc.vector.tensor_tensor(
+                    out=m1t[:], in0=acc_hje, in1=tab_je[:, 0, :, :, :].to_broadcast([P, HB, J, 2]), op=ALU.mult
+                )
+                nc.vector.tensor_tensor(
+                    out=m2t[:], in0=acc_hje[:, :, :, ::-1],
+                    in1=tab_je[:, 1, :, :, :].to_broadcast([P, HB, J, 2])[:, :, :, ::-1], op=ALU.mult,
+                )
                 sum_ps = psum2.tile([P, NB], F32, name="sum_ps")
                 nc.tensor.matmul(
-                    out=sum_ps[:], lhsT=ident[:], rhs=m1t[:].rearrange("p h e j -> p (h e j)"), start=True, stop=False
+                    out=sum_ps[:], lhsT=ident[:], rhs=m1t[:].rearrange("p h j e -> p (h j e)"), start=True, stop=False
                 )
                 nc.tensor.matmul(
-                    out=sum_ps[:], lhsT=ident[:], rhs=m2t[:].rearrange("p h e j -> p (h e j)"), start=False, stop=True
+                    out=sum_ps[:], lhsT=ident[:], rhs=m2t[:].rearrange("p h j e -> p (h j e)"), start=False, stop=True
                 )
                 sums[b] = sum_ps
                 return
             b0, cnt = run_of[b]
-            nh = HB * cnt
             h0 = HB * (b - b0)
-            if b0 in q_first:
-                if b == b0:
-                    m1q = work.tile([P, Q_MAX * HB, 2, J], F32, name="m1q")
-                    m2q = work.tile([P, Q_MAX * HB, 2, J], F32, name="m2q")
-                    runs[b0] = (m1q, m2q)
-                m1q, m2q = runs[b0]
-                wide(b, m1q[:, h0 : h0 + HB, :, :], m2q[:, h0 : h0 + HB, :, :])
-                if b == b0 + cnt - 1:
-                    sq = work.tile([P, Q_MAX * HB, 2, J], F32, name="sq")
-                    nc.gpsimd.tensor_tensor(
-                        out=sq[:, 0:nh, :, :], in0=m1q[:, 0:nh, :, :], in1=m2q[:, 0:nh, :, :], op=ALU.add
-                    )
-                    sums[b0] = sq
-                return
             if b == b0:
-                m1 = work.tile([P, P_MAX * HB, J, 2], F32, name="m1")
-                m2 = work.tile([P, P_MAX * HB, 2, J], F32, name="m2")
-                runs[b0] = (m1, m2)
-            m1, m2 = runs[b0]
+                m_new = work.tile([P, P_MAX * HB, 2, D], F32, name="m")
+                runs[b0] = m_new
+            m = runs[b0]
             rstd = rstds[b]
-            last = b == NBANKS - 1
             for h in range(HB):
-                acc_je = acc[:, D * h : D * (h + 1)].rearrange("p (j e) -> p j e", e=2)
                 nc.vector.scalar_tensor_tensor(
-                    out=m1[:, h0 + h, :, :], in0=acc_je, scalar=rstd[:, h : h + 1], in1=tab_a[:, i, :, :],
-                    op0=ALU.mult, op1=ALU.mult,
+                    out=m[:, h0 + h, :, :],
+                    in0=acc[:, D * h : D * (h + 1)].rearrange("p (o n) -> p o n", o=1).to_broadcast([P, 2, D]),
+                    scalar=rstd[:, h : h + 1], in1=tab[:, i, :, :], op0=ALU.mult, op1=ALU.mult,
                 )
-                for e in range(2):
-                    nc.vector.scalar_tensor_tensor(
-                        out=m2[:, h0 + h, e, :], in0=acc_je[:, :, 1 - e], scalar=rstd[:, h : h + 1],
-                        in1=tab_bd[:, i, e, :], op0=ALU.mult, op1=ALU.mult,
-                    )
-                if last and h == 0 - 1:
-                    add_heads(nc.gpsimd, b0, m1, m2, 0, 0)
-            if last:
-                add_heads(nc.vector, b0, m1, m2, 0, HB - 0)
+            if b == NBANKS - 1:
+                add_heads(nc.vector, b0, m, HB * cnt)
             elif b == b0 + cnt - 1:
-                add_heads(nc.gpsimd, b0, m1, m2, 0, nh)
+                add_heads(nc.gpsimd, b0, m, HB * cnt)
 
-        def scale_late(b0, cnt):
-            yl = work.tile([P, Q_MAX * HB, J, 2], F32, name="yl")
-            for b in range(b0, b0 + cnt):
-                for h in range(HB):
-                    hh = HB * (b - b0) + h
-                    if b0 in T_BANKS:
-                        src = sums[b0][:, D * h : D * (h + 1)].rearrange("p (e j) -> p j e", e=2)
-                    else:
-                        src = sums[b0][:, hh, :, :].rearrange("p e j -> p j e")
-                    nc.scalar.activation(out=yl[:, hh, :, :], in_=src, func=AF.Copy, scale=rstds[b][:, h : h + 1])
-            store(b0, 0, HB * cnt, yl[:, 0 : HB * cnt, :, :])
+        def scale_late(b):
+            yl = work.tile([P, HB, J, 2], F32, name="yl")
+            for h in range(HB):
+                nc.scalar.activation(
+                    out=yl[:, h, :, :].rearrange("p j e -> p (j e)"), in_=sums[b][:, D * h : D * (h + 1)],
+                    func=AF.Copy, scale=rstds[b][:, h : h + 1],
+                )
+            store(b, HB, yl[:])
 
-        for s in range(-LA, NBANKS + max(SC_T, SC_Q) + 1):
+        for s in range(-LA, NBANKS + SC_T + 1):
             a = s + LA
             if a < NBANKS:
                 mx(a)
                 if a not in V_FIRST:
                     sumsq(a)
             if s - SC_T in T_BANKS:
-                scale_late(s - SC_T, 1)
-            for (b0, cnt) in Q_RUNS:
-                if b0 + cnt - 1 == s - SC_Q:
-                    scale_late(b0, cnt)
+                scale_late(s - SC_T)
             if 0 <= s < NBANKS:
                 products(s)
                 if s in V_FIRST:

@@ -27,7 +27,7 @@ J = D // 2
 NBANKS = NT * NBK
 
 T_BANKS = (0, 4, 12, 16, 20, 24, 28)
-P_RUNS = ((1, 3), (5, 3), (8, 4), (13, 3), (17, 3), (21, 3), (25, 3), (29, 1), (30, 1), (31, 1))
+P_RUNS = ((1, 1), (2, 2), (5, 1), (6, 2), (8, 4), (13, 3), (17, 3), (21, 3), (25, 2), (27, 1), (29, 1), (30, 1), (31, 1))
 V_FIRST = (0,)
 P_MAX = 4
 NA = 6
@@ -40,6 +40,11 @@ XA = 2
 def tile_mla_pb_kernel(tc, x_words, x_scales, wq_words, wq_scales, q_norm_w, freqs_cos, freqs_sin, out):
     nc = tc.nc
     out2 = out.rearrange("b t h d -> (b t) (h d)")
+    SEQ = (
+        [(i, n) for i in range(XA) for n in (0, 1)]
+        + [(i, n) for i in range(XA) for n in (2, 3)]
+        + [(i, n) for i in range(XA, NT) for n in range(NBK)]
+    )
 
     with ExitStack() as ctx:
         const = ctx.enter_context(tc.tile_pool(name="const", bufs=1))
@@ -76,8 +81,6 @@ def tile_mla_pb_kernel(tc, x_words, x_scales, wq_words, wq_scales, q_norm_w, fre
         nc.gpsimd.memset(ones[:], 1.0)
         make_identity(nc, ident[:])
 
-        nc.sync.dma_start(out=trig[:, :, 0, :], in_=freqs_cos.rearrange("(i p) j -> p i j", p=P))
-        nc.sync.dma_start(out=trig[:, :, 1, :], in_=freqs_sin.rearrange("(i p) j -> p i j", p=P))
         nc.sync.dma_start(out=xca[:], in_=x_words[:, :, 0 : 2 * P * XA].rearrange("g p n -> p g n"))
         nc.sync.dma_start(out=wc[0][:], in_=wq_words[:, :, 0 : 2 * NB].rearrange("g p n -> p g n"))
 
@@ -95,6 +98,8 @@ def tile_mla_pb_kernel(tc, x_words, x_scales, wq_words, wq_scales, q_norm_w, fre
 
         load_scales(xsa, x_scales[:, :, 0 : P * XA])
         load_scales(wsa, wq_scales[:, :, 0 : N // 2])
+        nc.sync.dma_start(out=trig[:, :, 0, :], in_=freqs_cos.rearrange("(i p) j -> p i j", p=P))
+        nc.sync.dma_start(out=trig[:, :, 1, :], in_=freqs_sin.rearrange("(i p) j -> p i j", p=P))
         load_w(1)
         load_w(2)
         load_scales(wsb, wq_scales[:, :, N // 2 : N])
@@ -136,7 +141,7 @@ def tile_mla_pb_kernel(tc, x_words, x_scales, wq_words, wq_scales, q_norm_w, fre
                 run_of[b] = (b0, cnt)
 
         def mx(b):
-            i, n = divmod(b, NBK)
+            i, n = SEQ[b]
             acc = psum.tile([P, NB], F32, name="acc")
             accs[b] = acc
             for g in range(G):
@@ -172,7 +177,7 @@ def tile_mla_pb_kernel(tc, x_words, x_scales, wq_words, wq_scales, q_norm_w, fre
             )
 
         def store(b0, nh, y):
-            i, n = divmod(b0, NBK)
+            i, n = SEQ[b0]
             c0 = NB * n
             nc.sync.dma_start(out=out2[P * i : P * (i + 1), c0 : c0 + D * nh], in_=y.rearrange("p h j e -> p (h j e)"))
 
@@ -187,7 +192,7 @@ def tile_mla_pb_kernel(tc, x_words, x_scales, wq_words, wq_scales, q_norm_w, fre
             store(b0, nh, y[:, 0:nh, :, :])
 
         def products(b):
-            i, n = divmod(b, NBK)
+            i, n = SEQ[b]
             acc = accs[b]
             if b in T_BANKS:
                 m1t = work.tile([P, HB, J, 2], F32, name="m1t")

@@ -35,6 +35,8 @@ LA = 5
 SC_T = 3
 V_TILES = 2
 XA = 2
+WARM_A = 24
+WARM_B = 10
 
 
 def tile_mla_pb_kernel(tc, x_words, x_scales, wq_words, wq_scales, q_norm_w, freqs_cos, freqs_sin, out):
@@ -64,7 +66,8 @@ def tile_mla_pb_kernel(tc, x_words, x_scales, wq_words, wq_scales, q_norm_w, fre
         for n in range(NBK):
             wc_n = const.tile([P, G, 2 * NB], U8, name="wc%d" % n, align_bytes=64)
             wc.append(wc_n)
-        trig = const.tile([P, NT, 2, J], BF16, name="trig")
+        trig_a = const.tile([P, XA, 2, J], BF16, name="trig_a")
+        trig_b = const.tile([P, NT - XA, 2, J], BF16, name="trig_b")
         wrow = const.tile([P, 2 * D], BF16, name="wrow")
         ones = const.tile([P, P], BF16, name="ones")
         ident = const.tile([P, P], F32, name="ident")
@@ -73,12 +76,13 @@ def tile_mla_pb_kernel(tc, x_words, x_scales, wq_words, wq_scales, q_norm_w, fre
         w2 = const.tile([P, 2, J, 2], F32, name="w2")
         tab = const.tile([P, NT, 2, D], F32, name="tab")
 
-        for plane in (xsa, wsa, wsb, xsb):
+        nc.vector.memset(xsa[:].bitcast(I32), 0)
+        nc.vector.memset(ones[:], 1.0)
+        for plane in (wsa, wsb, xsb):
             nc.vector.memset(plane[:].bitcast(I32), 0)
         nc.vector.memset(eps_t[:], EPS)
         nc.gpsimd.memset(wrow[:], 0.0)
         nc.gpsimd.dma_start(out=wrow[0:1, 0:D], in_=q_norm_w.rearrange("(o d) -> o d", o=1))
-        nc.gpsimd.memset(ones[:], 1.0)
         make_identity(nc, ident[:])
 
         nc.sync.dma_start(out=xca[:], in_=x_words[:, :, 0 : 2 * P * XA].rearrange("g p n -> p g n"))
@@ -98,19 +102,28 @@ def tile_mla_pb_kernel(tc, x_words, x_scales, wq_words, wq_scales, q_norm_w, fre
 
         load_scales(xsa, x_scales[:, :, 0 : P * XA])
         load_scales(wsa, wq_scales[:, :, 0 : N // 2])
-        nc.sync.dma_start(out=trig[:, :, 0, :], in_=freqs_cos.rearrange("(i p) j -> p i j", p=P))
-        nc.sync.dma_start(out=trig[:, :, 1, :], in_=freqs_sin.rearrange("(i p) j -> p i j", p=P))
+        cos_pij = freqs_cos.rearrange("(i p) j -> p i j", p=P)
+        sin_pij = freqs_sin.rearrange("(i p) j -> p i j", p=P)
+        nc.sync.dma_start(out=trig_a[:, :, 0, :], in_=cos_pij[:, 0:XA, :])
+        nc.sync.dma_start(out=trig_a[:, :, 1, :], in_=sin_pij[:, 0:XA, :])
         load_w(1)
         load_w(2)
         load_scales(wsb, wq_scales[:, :, N // 2 : N])
         load_w(3)
+        nc.sync.dma_start(out=trig_b[:, :, 0, :], in_=cos_pij[:, XA:NT, :])
+        nc.sync.dma_start(out=trig_b[:, :, 1, :], in_=sin_pij[:, XA:NT, :])
         load_scales(xsb, x_scales[:, :, P * XA : T])
         nc.sync.dma_start(out=xcb[:], in_=x_words[:, :, 2 * P * XA : 2 * T].rearrange("g p n -> p g n"))
 
         nc.scalar.activation(out=dummy[:], in_=eps_t[:], func=AF.Abs_reciprocal_sqrt)
 
+        warm_ps = psum2.tile([P, NB], F32, name="sum_ps")
+        for k in range(WARM_A):
+            nc.tensor.matmul(out=warm_ps[:, 0:P], lhsT=ones[:], rhs=ones[:], start=True, stop=True)
         w_ps = psum2.tile([P, NB], F32, name="sum_ps")
         nc.tensor.matmul(out=w_ps[:, 0 : 2 * D], lhsT=ones[:], rhs=wrow[:], start=True, stop=True)
+        for k in range(WARM_B):
+            nc.tensor.matmul(out=warm_ps[:, 0:P], lhsT=ones[:], rhs=ones[:], start=True, stop=True)
         w_je = w_ps[:, 0:D].rearrange("p (j e) -> p j e", e=2)
         nc.vector.tensor_copy(out=w2[:, 0, :, :], in_=w_je)
         nc.vector.tensor_copy(out=w2[:, 1, :, 0:1], in_=w_je[:, :, 0:1])
@@ -120,9 +133,10 @@ def tile_mla_pb_kernel(tc, x_words, x_scales, wq_words, wq_scales, q_norm_w, fre
 
         def tables(eng, i0, i1):
             ni = i1 - i0
+            trig = trig_a[:, i0:i1, :, :] if i1 <= XA else trig_b[:, i0 - XA : i1 - XA, :, :]
             eng.tensor_tensor(
                 out=tab[:, i0:i1, :, :].rearrange("p i r (j e) -> p i (r j) e", e=2),
-                in0=trig[:, i0:i1, :, :].rearrange("p i r (j o) -> p i (r j) o", o=1).to_broadcast([P, ni, 2 * J, 2]),
+                in0=trig.rearrange("p i r (j o) -> p i (r j) o", o=1).to_broadcast([P, ni, 2 * J, 2]),
                 in1=w2[:].rearrange("p (o r) j e -> p o (r j) e", o=1).to_broadcast([P, ni, 2 * J, 2]),
                 op=ALU.mult,
             )

@@ -26,8 +26,9 @@ HB = NB // D
 J = D // 2
 NBANKS = NT * NBK
 
-T_BANKS = (0, 4, 12, 16, 20, 24, 28)
-P_RUNS = ((1, 1), (2, 2), (5, 1), (6, 2), (8, 4), (13, 3), (17, 3), (21, 3), (25, 2), (27, 1), (29, 1), (30, 1), (31, 1))
+T_BANKS = (8, 12, 16, 20, 24, 28)
+Q_BANKS = (0,)
+P_RUNS = ((1, 1), (2, 2), (4, 2), (6, 2), (9, 3), (13, 3), (17, 3), (21, 3), (25, 2), (27, 1), (29, 1), (30, 1), (31, 1))
 V_FIRST = (0,)
 P_MAX = 4
 NA = 6
@@ -208,7 +209,7 @@ def tile_mla_pb_kernel(tc, x_words, x_scales, wq_words, wq_scales, q_norm_w, fre
         def products(b):
             i, n = SEQ[b]
             acc = accs[b]
-            if b in T_BANKS:
+            if b in T_BANKS or b in Q_BANKS:
                 m1t = work.tile([P, HB, J, 2], F32, name="m1t")
                 m2t = work.tile([P, HB, J, 2], F32, name="m2t")
                 acc_hje = acc[:].rearrange("p (h j e) -> p h j e", h=HB, e=2)
@@ -220,6 +221,14 @@ def tile_mla_pb_kernel(tc, x_words, x_scales, wq_words, wq_scales, q_norm_w, fre
                     out=m2t[:], in0=acc_hje[:, :, :, ::-1],
                     in1=tab_je[:, 1, :, :, :].to_broadcast([P, HB, J, 2])[:, :, :, ::-1], op=ALU.mult,
                 )
+                if b in Q_BANKS:
+                    sum_sb = work.tile([P, NB], F32, name="sum_sb")
+                    nc.gpsimd.tensor_tensor(
+                        out=sum_sb[:], in0=m1t[:].rearrange("p h j e -> p (h j e)"),
+                        in1=m2t[:].rearrange("p h j e -> p (h j e)"), op=ALU.add,
+                    )
+                    sums[b] = sum_sb
+                    return
                 sum_ps = psum2.tile([P, NB], F32, name="sum_ps")
                 nc.tensor.matmul(
                     out=sum_ps[:], lhsT=ident[:], rhs=m1t[:].rearrange("p h j e -> p (h j e)"), start=True, stop=False
@@ -262,7 +271,7 @@ def tile_mla_pb_kernel(tc, x_words, x_scales, wq_words, wq_scales, q_norm_w, fre
                 mx(a)
                 if a not in V_FIRST:
                     sumsq(a)
-            if s - SC_T in T_BANKS:
+            if s - SC_T in T_BANKS or s - SC_T in Q_BANKS:
                 scale_late(s - SC_T)
             if 0 <= s < NBANKS:
                 products(s)

@@ -194,7 +194,8 @@ def tile_mla_pb_kernel(tc, x_words, x_scales, wq_words, wq_scales, q_norm_w, fre
         def store(b0, nh, y):
             i, n = SEQ[b0]
             c0 = NB * n
-            nc.sync.dma_start(out=out2[P * i : P * (i + 1), c0 : c0 + D * nh], in_=y.rearrange("p h j e -> p (h j e)"))
+            queue = nc.scalar if b0 in (NBANKS - NBK, NBANKS - 1) else nc.sync
+            queue.dma_start(out=out2[P * i : P * (i + 1), c0 : c0 + D * nh], in_=y.rearrange("p h j e -> p (h j e)"))
 
         def add_heads(eng, b0, m, nh):
             y = work.tile([P, P_MAX * HB, J, 2], F32, name="y")

@@ -28,7 +28,9 @@ NBANKS = NT * NBK
 
 T_BANKS = (8, 12, 16, 20, 24, 28)
 Q_BANKS = (0,)
-P_RUNS = ((1, 1), (2, 2), (4, 2), (6, 2), (9, 3), (13, 3), (17, 3), (21, 3), (25, 2), (27, 1), (29, 1), (30, 1), (31, 1))
+P_RUNS = (
+    (2,), (1, 3), (4, 6), (5, 7), (9, 10, 11), (13, 14, 15), (17, 18, 19), (21, 22, 23), (25, 26), (27,), (29,), (30,), (31,)
+)
 V_FIRST = (0,)
 P_MAX = 4
 NA = 6
@@ -44,8 +46,7 @@ def tile_mla_pb_kernel(tc, x_words, x_scales, wq_words, wq_scales, q_norm_w, fre
     nc = tc.nc
     out2 = out.rearrange("b t h d -> (b t) (h d)")
     SEQ = (
-        [(i, n) for i in range(XA) for n in (0, 1)]
-        + [(i, n) for i in range(XA) for n in (2, 3)]
+        [(i, n) for n in range(NBK) for i in range(XA)]
         + [(i, n) for i in range(XA, NT) for n in range(NBK)]
     )
 
@@ -151,9 +152,9 @@ def tile_mla_pb_kernel(tc, x_words, x_scales, wq_words, wq_scales, q_norm_w, fre
         sums = {}
         runs = {}
         run_of = {}
-        for (b0, cnt) in P_RUNS:
-            for b in range(b0, b0 + cnt):
-                run_of[b] = (b0, cnt)
+        for run in P_RUNS:
+            for k, b in enumerate(run):
+                run_of[b] = (run, k)
 
         def mx(b):
             i, n = SEQ[b]
@@ -239,9 +240,10 @@ def tile_mla_pb_kernel(tc, x_words, x_scales, wq_words, wq_scales, q_norm_w, fre
                 )
                 sums[b] = sum_ps
                 return
-            b0, cnt = run_of[b]
-            h0 = HB * (b - b0)
-            if b == b0:
+            run, k = run_of[b]
+            b0, cnt = run[0], len(run)
+            h0 = HB * k
+            if b0 not in runs:
                 m_new = work.tile([P, P_MAX * HB, 2, D], F32, name="m")
                 runs[b0] = m_new
             m = runs[b0]
@@ -254,7 +256,7 @@ def tile_mla_pb_kernel(tc, x_words, x_scales, wq_words, wq_scales, q_norm_w, fre
                 )
             if b == NBANKS - 1:
                 add_heads(nc.vector, b0, m, HB * cnt)
-            elif b == b0 + cnt - 1:
+            elif b == max(run):
                 add_heads(nc.gpsimd, b0, m, HB * cnt)
 
         def scale_late(b):

from contextlib import ExitStack
import math

import concourse.mybir as mybir
from concourse.masks import make_identity

T, C, H, D = 1024, 1024, 16, 128
N = H * D
EPS = 1e-6
FLOPS = 2 * T * C * N

F32 = mybir.dt.float32
BF16 = mybir.dt.bfloat16
U8 = mybir.dt.uint8
I32 = mybir.dt.int32
FP4 = mybir.dt.float4_e2m1fn_x4
AF = mybir.ActivationFunctionType
ALU = mybir.AluOpType

P = 128
G = C // 512
NT = T // P
NB = 512
NBK = N // NB
HB = NB // D
J = D // 2
NBANKS = NT * NBK

T_BANKS = (8, 12, 16, 20, 24, 28)
Q_BANKS = (0,)
P_RUNS = (
    (2,), (1, 3), (4, 6), (5, 7), (9, 10, 11), (13, 14, 15), (17, 18, 19), (21, 22, 23), (25, 26), (27,), (29,), (30,), (31,)
)
V_FIRST = (0,)
P_MAX = 4
NA = 6
LA = 5
SC_T = 3
V_TILES = 2
XA = 2
WARM_A = 24
WARM_B = 10


def tile_mla_pb_kernel(tc, x_words, x_scales, wq_words, wq_scales, q_norm_w, freqs_cos, freqs_sin, out):
    nc = tc.nc
    out2 = out.rearrange("b t h d -> (b t) (h d)")
    SEQ = (
        [(i, n) for n in range(NBK) for i in range(XA)]
        + [(i, n) for i in range(XA, NT) for n in range(NBK)]
    )

    with ExitStack() as ctx:
        const = ctx.enter_context(tc.tile_pool(name="const", bufs=1))
        work = ctx.enter_context(tc.tile_pool(name="work", bufs=5))
        stat = ctx.enter_context(tc.tile_pool(name="stat", bufs=4))
        psum = ctx.enter_context(tc.psum_pool(name="psum", bufs=NA))
        psum2 = ctx.enter_context(tc.psum_pool(name="psum2", bufs=8 - NA))
        ctx.enter_context(tc.manual_schedule())

        xca = const.tile([P, G, 2 * P * XA], U8, name="xca", align_bytes=64)
        xcb = const.tile([P, G, 2 * P * (NT - XA)], U8, name="xcb", align_bytes=64)
        xsa = const.tile([P, G, P * XA], U8, name="xsa", align_bytes=64)
        xsb = const.tile([P, G, T - P * XA], U8, name="xsb", align_bytes=64)
        wsa = const.tile([P, G, N // 2], U8, name="wsa", align_bytes=64)
        wsb = const.tile([P, G, N // 2], U8, name="wsb", align_bytes=64)
        wc = []
        for n in range(NBK):
            wc_n = const.tile([P, G, 2 * NB], U8, name="wc%d" % n, align_bytes=64)
            wc.append(wc_n)
        trig_a = const.tile([P, XA, 2, J], BF16, name="trig_a")
        trig_b = const.tile([P, NT - XA, 2, J], BF16, name="trig_b")
        wrow = const.tile([P, 2 * D], BF16, name="wrow")
        ones = const.tile([P, P], BF16, name="ones")
        ident = const.tile([P, P], F32, name="ident")
        eps_t = const.tile([P, 1], F32, name="eps_t")
        dummy = const.tile([P, 1], F32, name="dummy")
        w2 = const.tile([P, 2, J, 2], F32, name="w2")
        tab = const.tile([P, NT, 2, D], F32, name="tab")

        nc.vector.memset(xsa[:].bitcast(I32), 0)
        nc.vector.memset(ones[:], 1.0)
        for plane in (wsa, wsb, xsb):
            nc.vector.memset(plane[:].bitcast(I32), 0)
        nc.vector.memset(eps_t[:], EPS)
        nc.gpsimd.memset(wrow[:], 0.0)
        nc.gpsimd.dma_start(out=wrow[0:1, 0:D], in_=q_norm_w.rearrange("(o d) -> o d", o=1))
        make_identity(nc, ident[:])

        nc.sync.dma_start(out=xca[:], in_=x_words[:, :, 0 : 2 * P * XA].rearrange("g p n -> p g n"))
        nc.sync.dma_start(out=wc[0][:], in_=wq_words[:, :, 0 : 2 * NB].rearrange("g p n -> p g n"))

        def load_scales(plane, src):
            for q in range(4):
                nc.sync.dma_start(
                    out=plane[32 * q : 32 * q + 4, :, :].bitcast(I32),
                    in_=src[:, 4 * q : 4 * q + 4, :].rearrange("g r n -> r g n").bitcast(I32),
                )

        def load_w(n):
            nc.sync.dma_start(
                out=wc[n][:], in_=wq_words[:, :, 2 * NB * n : 2 * NB * (n + 1)].rearrange("g p n -> p g n")
            )

        load_scales(xsa, x_scales[:, :, 0 : P * XA])
        load_scales(wsa, wq_scales[:, :, 0 : N // 2])
        cos_pij = freqs_cos.rearrange("(i p) j -> p i j", p=P)
        sin_pij = freqs_sin.rearrange("(i p) j -> p i j", p=P)
        nc.sync.dma_start(out=trig_a[:, :, 0, :], in_=cos_pij[:, 0:XA, :])
        nc.sync.dma_start(out=trig_a[:, :, 1, :], in_=sin_pij[:, 0:XA, :])
        load_w(1)
        load_w(2)
        load_scales(wsb, wq_scales[:, :, N // 2 : N])
        load_w(3)
        nc.sync.dma_start(out=trig_b[:, :, 0, :], in_=cos_pij[:, XA:NT, :])
        nc.sync.dma_start(out=trig_b[:, :, 1, :], in_=sin_pij[:, XA:NT, :])
        load_scales(xsb, x_scales[:, :, P * XA : T])
        nc.sync.dma_start(out=xcb[:], in_=x_words[:, :, 2 * P * XA : 2 * T].rearrange("g p n -> p g n"))

        nc.scalar.activation(out=dummy[:], in_=eps_t[:], func=AF.Abs_reciprocal_sqrt)

        warm_ps = psum2.tile([P, NB], F32, name="sum_ps")
        for k in range(WARM_A):
            nc.tensor.matmul(out=warm_ps[:, 0:P], lhsT=ones[:], rhs=ones[:], start=True, stop=True)
        w_ps = psum2.tile([P, NB], F32, name="sum_ps")
        nc.tensor.matmul(out=w_ps[:, 0 : 2 * D], lhsT=ones[:], rhs=wrow[:], start=True, stop=True)
        for k in range(WARM_B):
            nc.tensor.matmul(out=warm_ps[:, 0:P], lhsT=ones[:], rhs=ones[:], start=True, stop=True)
        w_je = w_ps[:, 0:D].rearrange("p (j e) -> p j e", e=2)
        nc.vector.tensor_copy(out=w2[:, 0, :, :], in_=w_je)
        nc.vector.tensor_copy(out=w2[:, 1, :, 0:1], in_=w_je[:, :, 0:1])
        nc.vector.tensor_scalar(
            out=w2[:, 1, :, 1:2], in0=w_je[:, :, 1:2], scalar1=-1.0, scalar2=None, op0=ALU.mult
        )

        def tables(eng, i0, i1):
            ni = i1 - i0
            trig = trig_a[:, i0:i1, :, :] if i1 <= XA else trig_b[:, i0 - XA : i1 - XA, :, :]
            eng.tensor_tensor(
                out=tab[:, i0:i1, :, :].rearrange("p i r (j e) -> p i (r j) e", e=2),
                in0=trig.rearrange("p i r (j o) -> p i (r j) o", o=1).to_broadcast([P, ni, 2 * J, 2]),
                in1=w2[:].rearrange("p (o r) j e -> p o (r j) e", o=1).to_broadcast([P, ni, 2 * J, 2]),
                op=ALU.mult,
            )

        tables(nc.vector, 0, 1)
        tables(nc.vector, 1, V_TILES)
        tables(nc.gpsimd, V_TILES, NT)

        accs = {}
        rstds = {}
        sums = {}
        runs = {}
        run_of = {}
        for run in P_RUNS:
            for k, b in enumerate(run):
                run_of[b] = (run, k)

        def mx(b):
            i, n = SEQ[b]
            acc = psum.tile([P, NB], F32, name="acc")
            accs[b] = acc
            for g in range(G):
                if i < XA:
                    codes = xca[:, g, 2 * P * i : 2 * P * (i + 1)]
                    x_plane = xsa[:, g, P * i : P * (i + 1)]
                else:
                    codes = xcb[:, g, 2 * P * (i - XA) : 2 * P * (i - XA + 1)]
                    x_plane = xsb[:, g, P * (i - XA) : P * (i - XA + 1)]
                w_plane = (wsa, wsb)[n // 2][:, g, NB * (n % 2) : NB * (n % 2 + 1)]
                nc.tensor.matmul_mx(
                    out=acc[:],
                    lhsT=codes.bitcast(FP4),
                    lhsT_scale=x_plane,
                    rhs=wc[n][:, g, :].bitcast(FP4),
                    rhs_scale=w_plane,
                    start=(g == 0),
                    stop=(g == G - 1),
                )

        def sumsq(b):
            ss = stat.tile([P, HB], F32, name="ss")
            rstd = stat.tile([P, HB], F32, name="rstd", bufs=12)
            rstds[b] = rstd
            for h in range(HB):
                junk = work.tile([P, D], F32, name="junk")
                nc.scalar.activation(
                    out=junk[:], in_=accs[b][:, D * h : D * (h + 1)], func=AF.Square,
                    scale=1.0 / math.sqrt(D), accum_out=ss[:, h : h + 1],
                )
            nc.scalar.activation(
                out=rstd[:], in_=ss[:], func=AF.Abs_reciprocal_sqrt, bias=eps_t[:, 0:1], scale=1.0
            )

        def store(b0, nh, y):
            i, n = SEQ[b0]
            c0 = NB * n
            queue = nc.scalar if b0 in (NBANKS - NBK, NBANKS - 1) else nc.sync
            queue.dma_start(out=out2[P * i : P * (i + 1), c0 : c0 + D * nh], in_=y.rearrange("p h j e -> p (h j e)"))

        def add_heads(eng, b0, m, nh):
            y = work.tile([P, P_MAX * HB, J, 2], F32, name="y")
            eng.tensor_tensor(
                out=y[:, 0:nh, :, :],
                in0=m[:, 0:nh, 0, :].rearrange("p h (j e) -> p h j e", e=2),
                in1=m[:, 0:nh, 1, :].rearrange("p h (j e) -> p h j e", e=2)[:, :, :, ::-1],
                op=ALU.add,
            )
            store(b0, nh, y[:, 0:nh, :, :])

        def products(b):
            i, n = SEQ[b]
            acc = accs[b]
            if b in T_BANKS or b in Q_BANKS:
                m1t = work.tile([P, HB, J, 2], F32, name="m1t")
                m2t = work.tile([P, HB, J, 2], F32, name="m2t")
                acc_hje = acc[:].rearrange("p (h j e) -> p h j e", h=HB, e=2)
                tab_je = tab[:, i, :, :].rearrange("p r (o j e) -> p r o j e", o=1, e=2)
                nc.vector.tensor_tensor(
                    out=m1t[:], in0=acc_hje, in1=tab_je[:, 0, :, :, :].to_broadcast([P, HB, J, 2]), op=ALU.mult
                )
                nc.vector.tensor_tensor(
                    out=m2t[:], in0=acc_hje[:, :, :, ::-1],
                    in1=tab_je[:, 1, :, :, :].to_broadcast([P, HB, J, 2])[:, :, :, ::-1], op=ALU.mult,
                )
                if b in Q_BANKS:
                    sum_sb = work.tile([P, NB], F32, name="sum_sb")
                    nc.gpsimd.tensor_tensor(
                        out=sum_sb[:], in0=m1t[:].rearrange("p h j e -> p (h j e)"),
                        in1=m2t[:].rearrange("p h j e -> p (h j e)"), op=ALU.add,
                    )
                    sums[b] = sum_sb
                    return
                sum_ps = psum2.tile([P, NB], F32, name="sum_ps")
                nc.tensor.matmul(
                    out=sum_ps[:], lhsT=ident[:], rhs=m1t[:].rearrange("p h j e -> p (h j e)"), start=True, stop=False
                )
                nc.tensor.matmul(
                    out=sum_ps[:], lhsT=ident[:], rhs=m2t[:].rearrange("p h j e -> p (h j e)"), start=False, stop=True
                )
                sums[b] = sum_ps
                return
            run, k = run_of[b]
            b0, cnt = run[0], len(run)
            h0 = HB * k
            if b0 not in runs:
                m_new = work.tile([P, P_MAX * HB, 2, D], F32, name="m")
                runs[b0] = m_new
            m = runs[b0]
            rstd = rstds[b]
            for h in range(HB):
                nc.vector.scalar_tensor_tensor(
                    out=m[:, h0 + h, :, :],
                    in0=acc[:, D * h : D * (h + 1)].rearrange("p (o n) -> p o n", o=1).to_broadcast([P, 2, D]),
                    scalar=rstd[:, h : h + 1], in1=tab[:, i, :, :], op0=ALU.mult, op1=ALU.mult,
                )
            if b == NBANKS - 1:
                add_heads(nc.vector, b0, m, HB * cnt)
            elif b == max(run):
                add_heads(nc.gpsimd, b0, m, HB * cnt)

        def scale_late(b):
            yl = work.tile([P, HB, J, 2], F32, name="yl")
            for h in range(HB):
                nc.scalar.activation(
                    out=yl[:, h, :, :].rearrange("p j e -> p (j e)"), in_=sums[b][:, D * h : D * (h + 1)],
                    func=AF.Copy, scale=rstds[b][:, h : h + 1],
                )
            store(b, HB, yl[:])

        for s in range(-LA, NBANKS + SC_T + 1):
            a = s + LA
            if a < NBANKS:
                mx(a)
                if a not in V_FIRST:
                    sumsq(a)
            if s - SC_T in T_BANKS or s - SC_T in Q_BANKS:
                scale_late(s - SC_T)
            if 0 <= s < NBANKS:
                products(s)
                if s in V_FIRST:
                    sumsq(s)
